import numpy as np
import ml_dtypes


def mxq(x, axis, fmt="e4m3"):
    dtype, down = {"e4m3": (ml_dtypes.float8_e4m3fn, 7), "e5m2": (ml_dtypes.float8_e5m2, 14)}[fmt]
    v = np.moveaxis(np.asarray(x, np.float32).astype(ml_dtypes.bfloat16).astype(np.float64), axis, -1)
    blocks = v.reshape(v.shape[:-1] + (-1, 32))
    amax = np.abs(blocks).max(-1, keepdims=True)
    byte = np.maximum(np.where(amax > 0, np.frexp(amax)[1] - 1 + 127, 0) - down, 1)
    scale = np.exp2(byte - 127.0)
    codes = (blocks / scale).astype(np.float32).astype(dtype).astype(np.float64)
    return np.moveaxis((codes * scale).reshape(v.shape), -1, axis)


WIDE = False


def mx_kscale(k):
    if not WIDE:
        return np.ones(k)
    levels = np.array([10, -10, 5, -5, 0])
    if k % 512:
        return np.exp2(np.random.permutation(np.resize(levels, k // 32))).repeat(32)
    a = np.empty((k // 512, 16))
    for p in range(k // 512):
        a[p, :8] = np.random.permutation(np.resize(levels, 8))
        for g in range(8):
            far = levels[np.abs(levels - a[p, g]) >= 10]
            a[p, g + 8] = far[np.random.randint(len(far))]
    return np.exp2(a.ravel()).repeat(32)


BF16 = ml_dtypes.bfloat16


def bf(x):
    return np.asarray(x, np.float32).astype(BF16)


def f64(x):
    return np.asarray(x).astype(np.float64)


B, T, D, F = 2, 512, 512, 512
BINS = np.array([-1.5, -1.0, -0.5, 0.0, 0.5, 1.0, 1.5])
NB = BINS.shape[0] + 1
INDEX = 0


def draw0():
    s = mx_kscale(D)
    s = s / s[INDEX]
    return {"x": bf(np.random.standard_normal((B, T, D)) * s),
            "W": bf(np.random.standard_normal((NB, D, F)) * 0.5 / np.sqrt(D) / s[None, :, None])}


def core(x, W):
    x, W = f64(x), f64(W)
    y = x[..., INDEX]
    mem = np.sum(np.where(y[..., None] > BINS, 1.0, 0.0), axis=-1)
    xf = x.reshape(B * T, D)
    memf = mem.reshape(B * T)
    xq = mxq(xf, 1, "e4m3")
    Wq = mxq(W, 1, "e4m3")
    out = np.zeros((B * T, F))
    for k in range(NB):
        sel = np.where(memf == k, 1.0, 0.0)[:, None]
        out = out + sel * (xq @ Wq[k])
    return out.reshape(B, T, F)


def e4m3fn_bytes(y):
    return np.clip(np.asarray(y, np.float64), -448.0, 448.0).astype(np.float32).astype(ml_dtypes.float8_e4m3fn).view(np.uint8)


def e4m3fn_values(b):
    return np.asarray(b, np.uint8).view(ml_dtypes.float8_e4m3fn).astype(np.float64)


def setup_inputs():
    d = draw0()
    x0 = np.asarray(d['W']).astype(np.float64)
    s = (np.max(np.abs(x0), axis=(0, 2), keepdims=True) / 448.0).astype(np.float32)
    out = {}
    for k, v in d.items():
        if k == 'W':
            out['W_bytes'] = e4m3fn_bytes(x0 / s.astype(np.float64))
            out['W_scale'] = s
        else:
            out[k] = v
    return out


def reference(x, W_bytes, W_scale):
    return core(x, e4m3fn_values(W_bytes) * W_scale.astype(np.float64))

@@ -1,0 +1,377 @@
+from contextlib import ExitStack
+
+import concourse.mybir as mybir
+from concourse.masks import make_identity
+
+F32 = mybir.dt.float32
+BF16 = mybir.dt.bfloat16
+U32 = mybir.dt.uint32
+U8 = mybir.dt.uint8
+FP8 = mybir.dt.float8_e4m3fn
+FP8X4 = mybir.dt.float8_e4m3fn_x4
+ALU = mybir.AluOpType
+ACT = mybir.ActivationFunctionType
+AX = mybir.AxisListType
+
+P = 128
+TOK = 1024
+D = 512
+F = 512
+NE = 8
+NT = TOK // P
+NG = 4
+BINS = (-1.5, -1.0, -0.5, 0.0, 0.5, 1.0, 1.5)
+V = "V"
+S = "S"
+
+FLOPS = 2 * TOK * D * F * NE
+
+
+def tile_dispatchbyvariable_pa_kernel(tc, x, W_bytes, W_scale, out):
+    nc = tc.nc
+    with ExitStack() as ctx:
+        keep = ctx.enter_context(tc.tile_pool(name="keep", bufs=1))
+        psum = ctx.enter_context(tc.psum_pool(name="psum", bufs=1))
+        ctx.enter_context(tc.manual_schedule())
+
+        wscale = keep.tile([P, 4], F32, name="wscale")
+        nc.sync.dma_start(out=wscale[:], in_=W_scale.rearrange("o (p t) u -> p (o t u)", t=4))
+        wbytes = []
+        for q in range(NE // 2):
+            wbytes_q = keep.tile([P, 4, 2, F], U8, name="wbytes%d" % q)
+            wbytes.append(wbytes_q)
+        first_pair = W_bytes[0:2].rearrange("e (p t) n -> p t e n", t=4)
+        for t in range(4):
+            nc.sync.dma_start(out=wbytes[0][:, t, :, :], in_=first_pair[:, t, :, :])
+        x_nat = keep.tile([P, NT, D], BF16, name="x_nat")
+        x_view = x.rearrange("b t d -> (b t) d").rearrange("(i p) d -> p i d", p=P)
+        for j in range(NT // 2):
+            nc.sync.dma_start(out=x_nat[:, 2 * j : 2 * j + 2, :], in_=x_view[:, 2 * j : 2 * j + 2, :])
+        for e in range(2, NE):
+            nc.sync.dma_start(
+                out=wbytes[e // 2][:, :, e % 2, :],
+                in_=W_bytes[e].rearrange("(p t) n -> p t n", t=4),
+            )
+
+        ident = keep.tile([P, P], F32, name="ident")
+        make_identity(nc, ident[:])
+        bins = keep.tile([P, 7], F32, name="bins")
+        for j in range(7):
+            nc.vector.memset(bins[:, j : j + 1], BINS[j])
+        cmp = keep.tile([P, NT, 8], F32, name="cmp")
+        nc.vector.memset(cmp[:], 1.0)
+        warm = keep.tile([P, 1], F32, name="warm")
+        nc.scalar.activation(out=warm[:], in_=bins[:, 0:1], func=ACT.Copy)
+
+        wplanes = []
+        for q in range(NE // 2):
+            wplanes_q = keep.tile([P, 4, 2, F], BF16, name="wplanes%d" % q)
+            wplanes.append(wplanes_q)
+        wq = []
+        ws = []
+        for e in range(NE):
+            wq_e = keep.tile([P, F], U32, name="wq%d" % e, align_bytes=64)
+            ws_e = keep.tile([P, F], U8, name="ws%d" % e, align_bytes=64)
+            wq.append(wq_e)
+            ws.append(ws_e)
+        wil = {}
+
+        def widen(q, t, eng):
+            src = wbytes[q][:, t, :, :].rearrange("p e n -> p (e n)").bitcast(FP8)
+            dst = wplanes[q][:, t, :, :].rearrange("p e n -> p (e n)")
+            if eng == V:
+                nc.vector.tensor_scalar(out=dst, in0=src, scalar1=wscale[:, t : t + 1], scalar2=None, op0=ALU.mult)
+            else:
+                nc.scalar.activation(out=dst, in_=src, func=ACT.Copy, scale=wscale[:, t : t + 1])
+
+        def interleave_w(e, eng):
+            wil_e = keep.tile([P, 4 * F], BF16, name="wil%d" % e, align_bytes=64)
+            wil[e] = wil_e
+            dst = wil_e[:].rearrange("p (n t) -> p n t", t=4)
+            src = wplanes[e // 2][:, :, e % 2, :].rearrange("p t n -> p n t")
+            if eng == V:
+                nc.vector.tensor_copy(out=dst, in_=src)
+            else:
+                nc.scalar.copy(out=dst, in_=src)
+
+        def quantize_w(e):
+            nc.vector.quantize_mx(out=wq[e][:].bitcast(FP8X4), scales=ws[e][:], in_=wil[e][:])
+
+        msum = keep.tile([P, NT], F32, name="msum")
+        grp1 = keep.tile([P, NT], F32, name="grp1")
+        low = keep.tile([P, NT], F32, name="low")
+        diag = keep.tile([P, NT, P], F32, name="diag")
+        x_re = keep.tile([P, NT, 2, P], F32, name="x_re")
+        masked_ident = []
+        xm = []
+        xq = []
+        xs = []
+        for a in range(NG):
+            mi_a = keep.tile([P, NT, P], F32, name="mident%d" % a)
+            xm_a = keep.tile([P, 4 * TOK], BF16, name="xm%d" % a, align_bytes=64)
+            xq_a = keep.tile([P, TOK], U32, name="xq%d" % a, align_bytes=64)
+            xs_a = keep.tile([P, TOK], U8, name="xs%d" % a, align_bytes=64)
+            masked_ident.append(mi_a)
+            xm.append(xm_a)
+            xq.append(xq_a)
+            xs.append(xs_a)
+        x_words = x_nat[:].rearrange("p i d -> p (i d)").bitcast(F32)
+
+        def reorder(j, eng):
+            src = x_words[:, 512 * j : 512 * (j + 1)].rearrange("p (i w u) -> p i u w", i=2, u=2)
+            dst = x_re[:, 2 * j : 2 * j + 2, :, :]
+            if eng == V:
+                nc.vector.tensor_copy(out=dst, in_=src)
+            else:
+                nc.scalar.copy(out=dst, in_=src)
+
+        def bucket(k):
+            if k == 0:
+                nc.vector.tensor_tensor(
+                    out=cmp[:, :, 1:8],
+                    in0=x_nat[:, :, 0:1].to_broadcast([P, NT, 7]),
+                    in1=bins[:].unsqueeze(1).to_broadcast([P, NT, 7]),
+                    op=ALU.is_gt,
+                )
+            elif k == 1:
+                nc.vector.tensor_reduce(out=msum[:], in_=cmp[:], axis=AX.X, op=ALU.add)
+            elif k == 2:
+                nc.vector.scalar_tensor_tensor(
+                    out=grp1[:], in0=cmp[:, :, 4], scalar=-4.0, in1=msum[:], op0=ALU.mult, op1=ALU.add
+                )
+            else:
+                nc.vector.tensor_scalar(
+                    out=low[:], in0=cmp[:, :, 4], scalar1=-1.0, scalar2=1.0, op0=ALU.mult, op1=ALU.add
+                )
+
+        def make_diag():
+            nc.vector.tensor_tensor(
+                out=diag[:],
+                in0=ident[:].unsqueeze(1).to_broadcast([P, NT, P]),
+                in1=grp1[:].unsqueeze(2).to_broadcast([P, NT, P]),
+                op=ALU.mult,
+            )
+
+        def mask_ident(a):
+            nc.vector.tensor_scalar(
+                out=masked_ident[a][:], in0=diag[:], scalar1=float(a + 1), scalar2=None, op0=ALU.is_equal
+            )
+
+        tbank = {}
+
+        def transposes(a, j):
+            bank = psum.tile([P, 2, 2, P], F32, name="tb%d_%d" % (a, j), tag="bank%d" % (4 * (a % 2) + j))
+            tbank[(a, j)] = bank
+            for i2 in range(2):
+                i = 2 * j + i2
+                for u in range(2):
+                    nc.tensor.transpose(bank[:, i2, u, :], x_re[:, i, u, :], masked_ident[a][:, i, :])
+
+        def empty(a, j, eng):
+            dst = xm[a][:].bitcast(F32)[:, 512 * j : 512 * (j + 1)].rearrange("p (i r u) -> p i r u", i=2, u=2)
+            src = tbank[(a, j)][:].rearrange("p i u r -> p i r u")
+            if eng == V:
+                nc.vector.tensor_copy(out=dst, in_=src)
+            else:
+                nc.scalar.copy(out=dst, in_=src)
+
+        def quantize_x(a):
+            nc.vector.quantize_mx(out=xq[a][:].bitcast(FP8X4), scales=xs[a][:], in_=xm[a][:])
+
+        acc = {}
+
+        def multiply(e, i):
+            a = e % NG
+            if a == 0:
+                acc_i = psum.tile([P, F], F32, name="acc%d_%d" % (e, i), tag="bank%d" % i)
+                acc[i] = acc_i
+            cols = slice(P * i, P * (i + 1))
+            nc.tensor.matmul_mx(
+                out=acc[i][:],
+                lhsT=xq[a][:, cols].bitcast(FP8X4),
+                lhsT_scale=xs[a][:, cols],
+                rhs=wq[e][:].bitcast(FP8X4),
+                rhs_scale=ws[e][:],
+                start=(a == 0),
+                stop=(a == NG - 1),
+            )
+
+        part = {}
+        out_view = out.rearrange("b t f -> (b t) f").rearrange("(i p) f -> p i f", p=P)
+
+        def keep_low(i, eng):
+            part_i = keep.tile([P, F], F32, name="part%d" % i)
+            part[i] = part_i
+            if eng == V:
+                nc.vector.tensor_scalar(out=part_i[:], in0=acc[i][:], scalar1=low[:, i : i + 1], scalar2=None, op0=ALU.mult)
+            else:
+                nc.scalar.activation(out=part_i[:], in_=acc[i][:], func=ACT.Copy, scale=low[:, i : i + 1])
+
+        def finish(i):
+            res_i = keep.tile([P, F], F32, name="res%d" % i)
+            nc.vector.scalar_tensor_tensor(
+                out=res_i[:], in0=acc[i][:], scalar=cmp[:, i, 4:5], in1=part[i][:], op0=ALU.mult, op1=ALU.add
+            )
+            nc.sync.dma_start(out=out_view[:, i, :], in_=res_i[:])
+
+        widen(0, 1, V)
+        widen(0, 0, S)
+        widen(0, 2, V)
+        reorder(0, S)
+        widen(0, 3, V)
+        reorder(1, S)
+        reorder(2, S)
+        interleave_w(0, V)
+        bucket(0)
+        bucket(1)
+        reorder(3, S)
+        bucket(2)
+        make_diag()
+        widen(1, 0, S)
+        mask_ident(0)
+        transposes(0, 0)
+        mask_ident(1)
+        transposes(0, 1)
+        widen(1, 1, S)
+        transposes(0, 2)
+        mask_ident(2)
+        empty(0, 0, S)
+        transposes(0, 3)
+        transposes(1, 0)
+        mask_ident(3)
+        empty(0, 1, S)
+        transposes(1, 1)
+        transposes(1, 2)
+        empty(0, 2, S)
+        quantize_w(0)
+        transposes(1, 3)
+        empty(0, 3, S)
+        transposes(2, 0)
+        transposes(2, 1)
+        empty(1, 0, S)
+        transposes(2, 2)
+        interleave_w(1, V)
+        transposes(2, 3)
+        empty(1, 1, S)
+        transposes(3, 0)
+        empty(1, 2, S)
+        transposes(3, 1)
+        quantize_x(0)
+        transposes(3, 2)
+        empty(1, 3, S)
+        quantize_w(1)
+        transposes(3, 3)
+        widen(1, 2, S)
+        quantize_x(1)
+        bucket(3)
+        widen(2, 2, V)
+        widen(1, 3, S)
+        widen(2, 3, V)
+        empty(2, 0, S)
+        multiply(0, 0)
+        empty(2, 1, S)
+        multiply(1, 0)
+        multiply(0, 1)
+        empty(2, 2, S)
+        interleave_w(2, V)
+        multiply(1, 1)
+        multiply(0, 2)
+        empty(2, 3, S)
+        multiply(1, 2)
+        quantize_w(2)
+        multiply(0, 3)
+        empty(3, 0, S)
+        multiply(1, 3)
+        multiply(0, 4)
+        empty(3, 1, S)
+        multiply(1, 4)
+        quantize_x(2)
+        multiply(0, 5)
+        empty(3, 2, S)
+        multiply(1, 5)
+        multiply(0, 6)
+        empty(3, 3, S)
+        multiply(1, 6)
+        multiply(0, 7)
+        interleave_w(3, V)
+        multiply(1, 7)
+        multiply(2, 0)
+        widen(2, 0, S)
+        multiply(2, 1)
+        multiply(2, 2)
+        quantize_x(3)
+        multiply(2, 3)
+        multiply(2, 4)
+        multiply(2, 5)
+        quantize_w(3)
+        widen(2, 1, S)
+        multiply(2, 6)
+        multiply(2, 7)
+        widen(3, 1, V)
+        multiply(3, 0)
+        multiply(3, 1)
+        widen(3, 0, S)
+        multiply(3, 2)
+        multiply(3, 3)
+        multiply(3, 4)
+        interleave_w(4, V)
+        keep_low(0, S)
+        multiply(3, 5)
+        multiply(3, 6)
+        keep_low(1, S)
+        multiply(3, 7)
+        quantize_w(4)
+        multiply(4, 0)
+        keep_low(2, S)
+        multiply(4, 1)
+        multiply(4, 2)
+        keep_low(3, S)
+        interleave_w(5, V)
+        multiply(4, 3)
+        keep_low(4, S)
+        quantize_w(5)
+        keep_low(5, S)
+        multiply(5, 0)
+        multiply(4, 4)
+        widen(3, 2, V)
+        keep_low(6, S)
+        multiply(5, 1)
+        multiply(5, 2)
+        widen(3, 3, V)
+        keep_low(7, S)
+        multiply(4, 5)
+        multiply(5, 3)
+        multiply(4, 6)
+        multiply(5, 4)
+        multiply(4, 7)
+        interleave_w(6, V)
+        multiply(5, 5)
+        multiply(5, 6)
+        multiply(5, 7)
+        quantize_w(6)
+        multiply(6, 0)
+        multiply(6, 1)
+        multiply(6, 2)
+        multiply(6, 3)
+        interleave_w(7, V)
+        multiply(6, 4)
+        multiply(6, 5)
+        multiply(6, 6)
+        quantize_w(7)
+        multiply(6, 7)
+        multiply(7, 0)
+        multiply(7, 1)
+        multiply(7, 2)
+        finish(0)
+        multiply(7, 3)
+        multiply(7, 4)
+        finish(1)
+        multiply(7, 5)
+        multiply(7, 6)
+        finish(2)
+        multiply(7, 7)
+        finish(3)
+        finish(4)
+        finish(5)
+        finish(6)
+        finish(7)

@@ -1,10 +1,10 @@
 from contextlib import ExitStack
 
 import concourse.mybir as mybir
-from concourse.masks import make_identity
 
 F32 = mybir.dt.float32
 BF16 = mybir.dt.bfloat16
+I32 = mybir.dt.int32
 U32 = mybir.dt.uint32
 U8 = mybir.dt.uint8
 FP8 = mybir.dt.float8_e4m3fn
@@ -23,6 +23,7 @@ NG = 4
 BINS = (-1.5, -1.0, -0.5, 0.0, 0.5, 1.0, 1.5)
 V = "V"
 S = "S"
+IL_FAST = False
 
 FLOPS = 2 * TOK * D * F * NE
 
@@ -53,28 +54,30 @@ def tile_dispatchbyvariable_pa_kernel(tc, x, W_bytes, W_scale, out):
                 in_=W_bytes[e].rearrange("(p t) n -> p t n", t=4),
             )
 
-        ident = keep.tile([P, P], F32, name="ident")
-        make_identity(nc, ident[:])
+        col_minus_row = keep.tile([P, NG * P], I32, name="col_minus_row")
+        nc.gpsimd.iota(col_minus_row[:], pattern=[[1, NG * P]], base=0, channel_multiplier=-1)
         bins = keep.tile([P, 7], F32, name="bins")
         for j in range(7):
             nc.vector.memset(bins[:, j : j + 1], BINS[j])
-        cmp = keep.tile([P, NT, 8], F32, name="cmp")
-        nc.vector.memset(cmp[:], 1.0)
         warm = keep.tile([P, 1], F32, name="warm")
         nc.scalar.activation(out=warm[:], in_=bins[:, 0:1], func=ACT.Copy)
+        block_of_col = keep.tile([P, NG * P], F32, name="block_of_col")
+        nc.vector.tensor_scalar(out=block_of_col[:], in0=col_minus_row[:], scalar1=1.0 / P, scalar2=None, op0=ALU.mult)
 
         wplanes = []
         for q in range(NE // 2):
             wplanes_q = keep.tile([P, 4, 2, F], BF16, name="wplanes%d" % q)
             wplanes.append(wplanes_q)
+        wil = []
         wq = []
         ws = []
         for e in range(NE):
+            wil_e = keep.tile([P, 4 * F], BF16, name="wil%d" % e, align_bytes=64)
             wq_e = keep.tile([P, F], U32, name="wq%d" % e, align_bytes=64)
             ws_e = keep.tile([P, F], U8, name="ws%d" % e, align_bytes=64)
+            wil.append(wil_e)
             wq.append(wq_e)
             ws.append(ws_e)
-        wil = {}
 
         def widen(q, t, eng):
             src = wbytes[q][:, t, :, :].rearrange("p e n -> p (e n)").bitcast(FP8)
@@ -84,51 +87,48 @@ def tile_dispatchbyvariable_pa_kernel(tc, x, W_bytes, W_scale, out):
             else:
                 nc.scalar.activation(out=dst, in_=src, func=ACT.Copy, scale=wscale[:, t : t + 1])
 
-        def interleave_w(e, eng):
-            wil_e = keep.tile([P, 4 * F], BF16, name="wil%d" % e, align_bytes=64)
-            wil[e] = wil_e
-            dst = wil_e[:].rearrange("p (n t) -> p n t", t=4)
-            src = wplanes[e // 2][:, :, e % 2, :].rearrange("p t n -> p n t")
-            if eng == V:
-                nc.vector.tensor_copy(out=dst, in_=src)
+        def interleave_w(e):
+            if IL_FAST:
+                dst = wil[e][:].rearrange("p (c i t) -> p c t i", i=4, t=4)
+                src = wplanes[e // 2][:, :, e % 2, :].rearrange("p t (c i) -> p c t i", i=4)
             else:
-                nc.scalar.copy(out=dst, in_=src)
+                dst = wil[e][:].rearrange("p (n t) -> p n t", t=4)
+                src = wplanes[e // 2][:, :, e % 2, :].rearrange("p t n -> p n t")
+            nc.vector.tensor_copy(out=dst, in_=src)
 
         def quantize_w(e):
             nc.vector.quantize_mx(out=wq[e][:].bitcast(FP8X4), scales=ws[e][:], in_=wil[e][:])
 
+        cmp = keep.tile([P, NT, 7], F32, name="cmp")
         msum = keep.tile([P, NT], F32, name="msum")
-        grp1 = keep.tile([P, NT], F32, name="grp1")
+        grp = keep.tile([P, NT], F32, name="grp")
         low = keep.tile([P, NT], F32, name="low")
-        diag = keep.tile([P, NT, P], F32, name="diag")
         x_re = keep.tile([P, NT, 2, P], F32, name="x_re")
-        masked_ident = []
+        mident = []
         xm = []
         xq = []
         xs = []
-        for a in range(NG):
-            mi_a = keep.tile([P, NT, P], F32, name="mident%d" % a)
-            xm_a = keep.tile([P, 4 * TOK], BF16, name="xm%d" % a, align_bytes=64)
-            xq_a = keep.tile([P, TOK], U32, name="xq%d" % a, align_bytes=64)
-            xs_a = keep.tile([P, TOK], U8, name="xs%d" % a, align_bytes=64)
-            masked_ident.append(mi_a)
-            xm.append(xm_a)
-            xq.append(xq_a)
-            xs.append(xs_a)
+        for i in range(NT):
+            mident_i = keep.tile([P, NG * P], F32, name="mident%d" % i)
+            xm_i = keep.tile([P, NG * P * 4], BF16, name="xm%d" % i, align_bytes=64)
+            xq_i = keep.tile([P, NG * P], U32, name="xq%d" % i, align_bytes=64)
+            xs_i = keep.tile([P, NG * P], U8, name="xs%d" % i, align_bytes=64)
+            mident.append(mident_i)
+            xm.append(xm_i)
+            xq.append(xq_i)
+            xs.append(xs_i)
         x_words = x_nat[:].rearrange("p i d -> p (i d)").bitcast(F32)
 
-        def reorder(j, eng):
-            src = x_words[:, 512 * j : 512 * (j + 1)].rearrange("p (i w u) -> p i u w", i=2, u=2)
-            dst = x_re[:, 2 * j : 2 * j + 2, :, :]
-            if eng == V:
-                nc.vector.tensor_copy(out=dst, in_=src)
-            else:
-                nc.scalar.copy(out=dst, in_=src)
+        def reorder(j):
+            nc.scalar.copy(
+                out=x_re[:, 2 * j : 2 * j + 2, :, :],
+                in_=x_words[:, 512 * j : 512 * (j + 1)].rearrange("p (i w u) -> p i u w", i=2, u=2),
+            )
 
         def bucket(k):
             if k == 0:
                 nc.vector.tensor_tensor(
-                    out=cmp[:, :, 1:8],
+                    out=cmp[:],
                     in0=x_nat[:, :, 0:1].to_broadcast([P, NT, 7]),
                     in1=bins[:].unsqueeze(1).to_broadcast([P, NT, 7]),
                     op=ALU.is_gt,
@@ -137,46 +137,39 @@ def tile_dispatchbyvariable_pa_kernel(tc, x, W_bytes, W_scale, out):
                 nc.vector.tensor_reduce(out=msum[:], in_=cmp[:], axis=AX.X, op=ALU.add)
             elif k == 2:
                 nc.vector.scalar_tensor_tensor(
-                    out=grp1[:], in0=cmp[:, :, 4], scalar=-4.0, in1=msum[:], op0=ALU.mult, op1=ALU.add
+                    out=grp[:], in0=cmp[:, :, 3], scalar=-4.0, in1=msum[:], op0=ALU.mult, op1=ALU.add
                 )
             else:
                 nc.vector.tensor_scalar(
-                    out=low[:], in0=cmp[:, :, 4], scalar1=-1.0, scalar2=1.0, op0=ALU.mult, op1=ALU.add
+                    out=low[:], in0=cmp[:, :, 3], scalar1=-1.0, scalar2=1.0, op0=ALU.mult, op1=ALU.add
                 )
 
-        def make_diag():
-            nc.vector.tensor_tensor(
-                out=diag[:],
-                in0=ident[:].unsqueeze(1).to_broadcast([P, NT, P]),
-                in1=grp1[:].unsqueeze(2).to_broadcast([P, NT, P]),
-                op=ALU.mult,
-            )
-
-        def mask_ident(a):
+        def mask_identity(i):
             nc.vector.tensor_scalar(
-                out=masked_ident[a][:], in0=diag[:], scalar1=float(a + 1), scalar2=None, op0=ALU.is_equal
+                out=mident[i][:], in0=block_of_col[:], scalar1=grp[:, i : i + 1], scalar2=None, op0=ALU.is_equal
             )
 
         tbank = {}
 
-        def transposes(a, j):
-            bank = psum.tile([P, 2, 2, P], F32, name="tb%d_%d" % (a, j), tag="bank%d" % (4 * (a % 2) + j))
-            tbank[(a, j)] = bank
-            for i2 in range(2):
-                i = 2 * j + i2
-                for u in range(2):
-                    nc.tensor.transpose(bank[:, i2, u, :], x_re[:, i, u, :], masked_ident[a][:, i, :])
+        def transposes(i):
+            for h in range(2):
+                bank = psum.tile([P, 2, 2, P], F32, name="tb%d_%d" % (i, h), tag="bank%d" % (4 + (2 * i + h) % 4))
+                tbank[(i, h)] = bank
+                for a2 in range(2):
+                    a = 2 * h + a2
+                    for u in range(2):
+                        nc.tensor.transpose(bank[:, a2, u, :], x_re[:, i, u, :], mident[i][:, P * a : P * (a + 1)])
 
-        def empty(a, j, eng):
-            dst = xm[a][:].bitcast(F32)[:, 512 * j : 512 * (j + 1)].rearrange("p (i r u) -> p i r u", i=2, u=2)
-            src = tbank[(a, j)][:].rearrange("p i u r -> p i r u")
-            if eng == V:
-                nc.vector.tensor_copy(out=dst, in_=src)
-            else:
-                nc.scalar.copy(out=dst, in_=src)
+        def empty(i):
+            xm_words = xm[i][:].bitcast(F32)
+            for h in range(2):
+                nc.scalar.copy(
+                    out=xm_words[:, 512 * h : 512 * (h + 1)].rearrange("p (a r u) -> p a r u", a=2, u=2),
+                    in_=tbank[(i, h)][:].rearrange("p a u r -> p a r u"),
+                )
 
-        def quantize_x(a):
-            nc.vector.quantize_mx(out=xq[a][:].bitcast(FP8X4), scales=xs[a][:], in_=xm[a][:])
+        def quantize_x(i):
+            nc.vector.quantize_mx(out=xq[i][:].bitcast(FP8X4), scales=xs[i][:], in_=xm[i][:])
 
         acc = {}
 
@@ -185,11 +178,11 @@ def tile_dispatchbyvariable_pa_kernel(tc, x, W_bytes, W_scale, out):
             if a == 0:
                 acc_i = psum.tile([P, F], F32, name="acc%d_%d" % (e, i), tag="bank%d" % i)
                 acc[i] = acc_i
-            cols = slice(P * i, P * (i + 1))
+            cols = slice(P * a, P * (a + 1))
             nc.tensor.matmul_mx(
                 out=acc[i][:],
-                lhsT=xq[a][:, cols].bitcast(FP8X4),
-                lhsT_scale=xs[a][:, cols],
+                lhsT=xq[i][:, cols].bitcast(FP8X4),
+                lhsT_scale=xs[i][:, cols],
                 rhs=wq[e][:].bitcast(FP8X4),
                 rhs_scale=ws[e][:],
                 start=(a == 0),
@@ -199,179 +192,80 @@ def tile_dispatchbyvariable_pa_kernel(tc, x, W_bytes, W_scale, out):
         part = {}
         out_view = out.rearrange("b t f -> (b t) f").rearrange("(i p) f -> p i f", p=P)
 
-        def keep_low(i, eng):
+        def keep_low(i):
             part_i = keep.tile([P, F], F32, name="part%d" % i)
             part[i] = part_i
-            if eng == V:
-                nc.vector.tensor_scalar(out=part_i[:], in0=acc[i][:], scalar1=low[:, i : i + 1], scalar2=None, op0=ALU.mult)
-            else:
-                nc.scalar.activation(out=part_i[:], in_=acc[i][:], func=ACT.Copy, scale=low[:, i : i + 1])
+            nc.scalar.activation(out=part_i[:], in_=acc[i][:], func=ACT.Copy, scale=low[:, i : i + 1])
 
         def finish(i):
             res_i = keep.tile([P, F], F32, name="res%d" % i)
             nc.vector.scalar_tensor_tensor(
-                out=res_i[:], in0=acc[i][:], scalar=cmp[:, i, 4:5], in1=part[i][:], op0=ALU.mult, op1=ALU.add
+                out=res_i[:], in0=acc[i][:], scalar=cmp[:, i, 3:4], in1=part[i][:], op0=ALU.mult, op1=ALU.add
             )
             nc.sync.dma_start(out=out_view[:, i, :], in_=res_i[:])
 
-        widen(0, 1, V)
+        def two_experts(e, skew):
+            for d in range(NT + skew):
+                if d < NT:
+                    multiply(e, d)
+                if 0 <= d - skew:
+                    multiply(e + 1, d - skew)
+                    if e + 1 == NE - 1:
+                        finish(d - skew)
+
         widen(0, 0, S)
-        widen(0, 2, V)
-        reorder(0, S)
-        widen(0, 3, V)
-        reorder(1, S)
-        reorder(2, S)
-        interleave_w(0, V)
-        bucket(0)
-        bucket(1)
-        reorder(3, S)
-        bucket(2)
-        make_diag()
+        for t in (1, 2, 3):
+            widen(0, t, V)
+        for j in range(NT // 2):
+            reorder(j)
+        interleave_w(0)
+        for k in range(3):
+            bucket(k)
         widen(1, 0, S)
-        mask_ident(0)
-        transposes(0, 0)
-        mask_ident(1)
-        transposes(0, 1)
-        widen(1, 1, S)
-        transposes(0, 2)
-        mask_ident(2)
-        empty(0, 0, S)
-        transposes(0, 3)
-        transposes(1, 0)
-        mask_ident(3)
-        empty(0, 1, S)
-        transposes(1, 1)
-        transposes(1, 2)
-        empty(0, 2, S)
+        for i in range(NT):
+            mask_identity(i)
+        for i in range(NT):
+            if i == 4:
+                widen(1, 1, S)
+            transposes(i)
+            empty(i)
         quantize_w(0)
-        transposes(1, 3)
-        empty(0, 3, S)
-        transposes(2, 0)
-        transposes(2, 1)
-        empty(1, 0, S)
-        transposes(2, 2)
-        interleave_w(1, V)
-        transposes(2, 3)
-        empty(1, 1, S)
-        transposes(3, 0)
-        empty(1, 2, S)
-        transposes(3, 1)
-        quantize_x(0)
-        transposes(3, 2)
-        empty(1, 3, S)
+        interleave_w(1)
+        for i in range(4):
+            quantize_x(i)
         quantize_w(1)
-        transposes(3, 3)
-        widen(1, 2, S)
-        quantize_x(1)
-        bucket(3)
-        widen(2, 2, V)
-        widen(1, 3, S)
-        widen(2, 3, V)
-        empty(2, 0, S)
-        multiply(0, 0)
-        empty(2, 1, S)
-        multiply(1, 0)
-        multiply(0, 1)
-        empty(2, 2, S)
-        interleave_w(2, V)
-        multiply(1, 1)
-        multiply(0, 2)
-        empty(2, 3, S)
-        multiply(1, 2)
+        for e in (0, 1):
+            for i in range(4):
+                multiply(e, i)
+        widen(1, 2, V)
+        widen(1, 3, V)
+        interleave_w(2)
+        for i in range(4, NT):
+            quantize_x(i)
         quantize_w(2)
-        multiply(0, 3)
-        empty(3, 0, S)
-        multiply(1, 3)
-        multiply(0, 4)
-        empty(3, 1, S)
-        multiply(1, 4)
-        quantize_x(2)
-        multiply(0, 5)
-        empty(3, 2, S)
-        multiply(1, 5)
-        multiply(0, 6)
-        empty(3, 3, S)
-        multiply(1, 6)
-        multiply(0, 7)
-        interleave_w(3, V)
-        multiply(1, 7)
-        multiply(2, 0)
-        widen(2, 0, S)
-        multiply(2, 1)
-        multiply(2, 2)
-        quantize_x(3)
-        multiply(2, 3)
-        multiply(2, 4)
-        multiply(2, 5)
+        for e in (0, 1):
+            for i in range(4, NT):
+                multiply(e, i)
+        for q, t in ((2, 0), (2, 1), (2, 2), (3, 0), (3, 1)):
+            widen(q, t, S)
+        for i in range(NT):
+            multiply(2, i)
+        interleave_w(3)
+        widen(2, 3, V)
+        bucket(3)
         quantize_w(3)
-        widen(2, 1, S)
-        multiply(2, 6)
-        multiply(2, 7)
-        widen(3, 1, V)
-        multiply(3, 0)
-        multiply(3, 1)
-        widen(3, 0, S)
-        multiply(3, 2)
-        multiply(3, 3)
-        multiply(3, 4)
-        interleave_w(4, V)
-        keep_low(0, S)
-        multiply(3, 5)
-        multiply(3, 6)
-        keep_low(1, S)
-        multiply(3, 7)
-        quantize_w(4)
-        multiply(4, 0)
-        keep_low(2, S)
-        multiply(4, 1)
-        multiply(4, 2)
-        keep_low(3, S)
-        interleave_w(5, V)
-        multiply(4, 3)
-        keep_low(4, S)
-        quantize_w(5)
-        keep_low(5, S)
-        multiply(5, 0)
-        multiply(4, 4)
+        for i in range(NT):
+            multiply(3, i)
+            keep_low(i)
+        interleave_w(4)
         widen(3, 2, V)
-        keep_low(6, S)
-        multiply(5, 1)
-        multiply(5, 2)
+        quantize_w(4)
+        interleave_w(5)
         widen(3, 3, V)
-        keep_low(7, S)
-        multiply(4, 5)
-        multiply(5, 3)
-        multiply(4, 6)
-        multiply(5, 4)
-        multiply(4, 7)
-        interleave_w(6, V)
-        multiply(5, 5)
-        multiply(5, 6)
-        multiply(5, 7)
+        quantize_w(5)
+        two_experts(4, 4)
+        interleave_w(6)
+        interleave_w(7)
         quantize_w(6)
-        multiply(6, 0)
-        multiply(6, 1)
-        multiply(6, 2)
-        multiply(6, 3)
-        interleave_w(7, V)
-        multiply(6, 4)
-        multiply(6, 5)
-        multiply(6, 6)
         quantize_w(7)
-        multiply(6, 7)
-        multiply(7, 0)
-        multiply(7, 1)
-        multiply(7, 2)
-        finish(0)
-        multiply(7, 3)
-        multiply(7, 4)
-        finish(1)
-        multiply(7, 5)
-        multiply(7, 6)
-        finish(2)
-        multiply(7, 7)
-        finish(3)
-        finish(4)
-        finish(5)
-        finish(6)
-        finish(7)
+        two_experts(6, 1)

@@ -21,38 +21,141 @@ NE = 8
 NT = TOK // P
 NG = 4
 BINS = (-1.5, -1.0, -0.5, 0.0, 0.5, 1.0, 1.5)
-V = "V"
-S = "S"
-IL_FAST = False
 
 FLOPS = 2 * TOK * D * F * NE
 
 
+def plan():
+    LOADS = [('y', 16), ('x0', 256), ('wscale', 2)] + [('w0_%d' % t, 128) for t in range(4)] + [('x1', 256), ('we2', 256), ('we3', 256), ('x2', 256), ('we4', 256), ('we5', 256), ('x3', 256), ('we6', 256), ('we7', 256)]
+    def T(k, l): return [(k, i) for i in l]
+    def M(es, tiles): return [('mm', e, i) for e in es for i in tiles]
+    V = T('buck', (0, 1, 2)) + T('mask', range(4)) + [('wid', 0, 1), ('wid', 0, 2), ('wid', 0, 3), ('il', 0)] + T('mask', range(4, 8))
+    V += [('qx', 0), ('qx', 1), ('qw', 0), ('il', 1), ('qx', 2), ('qx', 3), ('qw', 1), ('wid', 1, 2), ('wid', 1, 3), ('qx', 4), ('qx', 5), ('il', 2), ('qx', 6), ('qx', 7), ('qw', 2), ('il', 3), ('wid', 2, 3), ('qw', 3)]
+    V += [('il', 4), ('wid', 3, 2), ('qw', 4), ('il', 5), ('wid', 3, 3), ('qw', 5), ('il', 6), ('il', 7), ('qw', 6), ('qw', 7)] + T('fin', range(8))
+    S = [('wid', 0, 0), ('emp', 0), ('emp', 1), ('wid', 1, 0), ('emp', 2), ('emp', 3), ('wid', 1, 1)] + T('emp', range(4, 8))
+    S += [('wid', 2, 0), ('wid', 2, 1), ('wid', 2, 2), ('wid', 3, 0), ('wid', 3, 1)] + T('low', range(8))
+    def zipped(e, skew):
+        r = []
+        for d in range(8 + skew):
+            if d < 8: r.append(('mm', e, d))
+            if d >= skew: r.append(('mm', e + 1, d - skew))
+        return r
+    P = T('tr', range(6)) + M((0,), range(4)) + T('tr', (6, 7)) + M((1,), range(4)) + M((0, 1), range(4, 8)) + M((2, 3), range(8)) + zipped(4, 5) + zipped(6, 1)
+    QUEUES = {'V': V, 'S': S, 'P': P, 'G': [('buck', 3)]}
+    LOADS = [n for n, kib in LOADS]
+    OPT = {"trb": (4, 5, 6, 7), "reorder": False, "pairs2": ()}
+    return LOADS, QUEUES, OPT
+
+
+def halves(queues):
+    out = {}
+    for eng in queues:
+        out[eng] = []
+        for st in queues[eng]:
+            if st[0] in ("tr", "emp") and len(st) == 2:
+                out[eng].extend([(st[0], st[1], 0), (st[0], st[1], 1)])
+            else:
+                out[eng].append(st)
+    return out
+
+
+def needs(st, trb, reorder):
+    k = st[0]
+    if k == "il":
+        return [("wid", st[1] // 2, t) for t in range(4)]
+    if k == "qw":
+        return [("il", st[1])]
+    if k == "buck":
+        return [] if st[1] == 0 else [("buck", 0)] if st[1] in (1, 3) else [("buck", 1)]
+    if k == "mask":
+        return [("buck", 2)]
+    if k == "tr":
+        j = 2 * st[1] + st[2] - len(trb)
+        return [("mask", st[1])] + ([("reo", st[1] // 2)] if reorder else []) + ([("emp", j // 2, j % 2)] if j >= 0 else [])
+    if k == "emp":
+        return [("tr", st[1], st[2])]
+    if k == "qx":
+        return [("emp", st[1], 0), ("emp", st[1], 1)]
+    if k == "mm":
+        r = [("qx", st[2]), ("qw", st[1])]
+        if st[1] < 4 and st[2] in trb:
+            r.extend([("emp", j // 2, j % 2) for j in range(16) if trb[j % len(trb)] == st[2]][-1:])
+        if st[1] >= 4:
+            r.append(("low", st[2]))
+        return r
+    if k == "low":
+        return [("mm", e, st[1]) for e in range(4)] + [("buck", 3)]
+    if k == "fin":
+        return [("mm", e, st[1]) for e in range(4, 8)] + [("low", st[1])]
+    if k == "hi":
+        return [("mm", e, st[1]) for e in range(4, 8)]
+    if k == "add":
+        return [("hi", st[1]), ("low", st[1])]
+    return []
+
+
+def merge(queues, trb, reorder):
+    pos = {}
+    for eng in queues:
+        pos[eng] = 0
+    emitted = set()
+    text = []
+    for rounds in range(10000):
+        moved = False
+        for eng in queues:
+            for tries in range(len(queues[eng])):
+                if pos[eng] >= len(queues[eng]):
+                    break
+                st = queues[eng][pos[eng]]
+                if not all(n in emitted for n in needs(st, trb, reorder)):
+                    break
+                text.append((eng, st))
+                emitted.add(st)
+                pos[eng] = pos[eng] + 1
+                moved = True
+        if not moved:
+            break
+    assert all(pos[eng] == len(queues[eng]) for eng in queues), "the queues block each other"
+    return text
+
+
 def tile_dispatchbyvariable_pa_kernel(tc, x, W_bytes, W_scale, out):
     nc = tc.nc
+    loads, queues, opt = plan()
+    queues = halves(queues)
+    trb = opt["trb"]
+    reorder = opt["reorder"]
+    pairs2 = opt["pairs2"]
     with ExitStack() as ctx:
         keep = ctx.enter_context(tc.tile_pool(name="keep", bufs=1))
         psum = ctx.enter_context(tc.psum_pool(name="psum", bufs=1))
         ctx.enter_context(tc.manual_schedule())
 
         wscale = keep.tile([P, 4], F32, name="wscale")
-        nc.sync.dma_start(out=wscale[:], in_=W_scale.rearrange("o (p t) u -> p (o t u)", t=4))
         wbytes = []
         for q in range(NE // 2):
             wbytes_q = keep.tile([P, 4, 2, F], U8, name="wbytes%d" % q)
             wbytes.append(wbytes_q)
-        first_pair = W_bytes[0:2].rearrange("e (p t) n -> p t e n", t=4)
-        for t in range(4):
-            nc.sync.dma_start(out=wbytes[0][:, t, :, :], in_=first_pair[:, t, :, :])
         x_nat = keep.tile([P, NT, D], BF16, name="x_nat")
         x_view = x.rearrange("b t d -> (b t) d").rearrange("(i p) d -> p i d", p=P)
-        for j in range(NT // 2):
-            nc.sync.dma_start(out=x_nat[:, 2 * j : 2 * j + 2, :], in_=x_view[:, 2 * j : 2 * j + 2, :])
-        for e in range(2, NE):
-            nc.sync.dma_start(
-                out=wbytes[e // 2][:, :, e % 2, :],
-                in_=W_bytes[e].rearrange("(p t) n -> p t n", t=4),
-            )
+        yt = keep.tile([P, NT, 2], BF16, name="yt")
+        first_pair = W_bytes[0:2].rearrange("e (p t) n -> p t e n", t=4)
+        use_y = False
+        for name in loads:
+            if name == "y":
+                use_y = True
+                nc.sync.dma_start(out=yt[:], in_=x_view[:, :, 0:2])
+            elif name == "wscale":
+                nc.sync.dma_start(out=wscale[:], in_=W_scale.rearrange("o (p t) u -> p (o t u)", t=4))
+            elif name.startswith("w0"):
+                t = int(name[3:])
+                nc.sync.dma_start(out=wbytes[0][:, t, :, :], in_=first_pair[:, t, :, :])
+            elif name.startswith("we"):
+                e = int(name[2:])
+                nc.sync.dma_start(out=wbytes[e // 2][:, :, e % 2, :], in_=W_bytes[e].rearrange("(p t) n -> p t n", t=4))
+            else:
+                j = int(name[1:])
+                nc.sync.dma_start(out=x_nat[:, 2 * j : 2 * j + 2, :], in_=x_view[:, 2 * j : 2 * j + 2, :])
 
         col_minus_row = keep.tile([P, NG * P], I32, name="col_minus_row")
         nc.gpsimd.iota(col_minus_row[:], pattern=[[1, NG * P]], base=0, channel_multiplier=-1)
@@ -66,7 +169,7 @@ def tile_dispatchbyvariable_pa_kernel(tc, x, W_bytes, W_scale, out):
 
         wplanes = []
         for q in range(NE // 2):
-            wplanes_q = keep.tile([P, 4, 2, F], BF16, name="wplanes%d" % q)
+            wplanes_q = keep.tile([P, 4 * 2 * F], BF16, name="wplanes%d" % q)
             wplanes.append(wplanes_q)
         wil = []
         wq = []
@@ -79,22 +182,28 @@ def tile_dispatchbyvariable_pa_kernel(tc, x, W_bytes, W_scale, out):
             wq.append(wq_e)
             ws.append(ws_e)
 
-        def widen(q, t, eng):
+        def widen(eng, q, t):
             src = wbytes[q][:, t, :, :].rearrange("p e n -> p (e n)").bitcast(FP8)
-            dst = wplanes[q][:, t, :, :].rearrange("p e n -> p (e n)")
-            if eng == V:
+            if q in pairs2:
+                dst = wplanes[q][:].rearrange("p (u m v) -> p u m v", u=2, v=2)[:, t // 2, :, t % 2]
+            else:
+                dst = wplanes[q][:].rearrange("p (t m) -> p t m", t=4)[:, t, :]
+            if eng == "V":
                 nc.vector.tensor_scalar(out=dst, in0=src, scalar1=wscale[:, t : t + 1], scalar2=None, op0=ALU.mult)
             else:
                 nc.scalar.activation(out=dst, in_=src, func=ACT.Copy, scale=wscale[:, t : t + 1])
 
-        def interleave_w(e):
-            if IL_FAST:
-                dst = wil[e][:].rearrange("p (c i t) -> p c t i", i=4, t=4)
-                src = wplanes[e // 2][:, :, e % 2, :].rearrange("p t (c i) -> p c t i", i=4)
+        def interleave_w(eng, e):
+            if e // 2 in pairs2:
+                dst = wil[e][:].bitcast(F32).rearrange("p (n u) -> p n u", u=2)
+                src = wplanes[e // 2][:].bitcast(F32).rearrange("p (u e n) -> p u e n", u=2, e=2)[:, :, e % 2, :].rearrange("p u n -> p n u")
             else:
                 dst = wil[e][:].rearrange("p (n t) -> p n t", t=4)
-                src = wplanes[e // 2][:, :, e % 2, :].rearrange("p t n -> p n t")
-            nc.vector.tensor_copy(out=dst, in_=src)
+                src = wplanes[e // 2][:].rearrange("p (t e n) -> p t e n", t=4, e=2)[:, :, e % 2, :].rearrange("p t n -> p n t")
+            if eng == "V":
+                nc.vector.tensor_copy(out=dst, in_=src)
+            else:
+                nc.scalar.copy(out=dst, in_=src)
 
         def quantize_w(e):
             nc.vector.quantize_mx(out=wq[e][:].bitcast(FP8X4), scales=ws[e][:], in_=wil[e][:])
@@ -119,17 +228,18 @@ def tile_dispatchbyvariable_pa_kernel(tc, x, W_bytes, W_scale, out):
             xs.append(xs_i)
         x_words = x_nat[:].rearrange("p i d -> p (i d)").bitcast(F32)
 
-        def reorder(j):
+        def reorder_x(j):
             nc.scalar.copy(
                 out=x_re[:, 2 * j : 2 * j + 2, :, :],
                 in_=x_words[:, 512 * j : 512 * (j + 1)].rearrange("p (i w u) -> p i u w", i=2, u=2),
             )
 
-        def bucket(k):
+        def bucket(eng, k):
             if k == 0:
+                first = yt[:, :, 0:1] if use_y else x_nat[:, :, 0:1]
                 nc.vector.tensor_tensor(
                     out=cmp[:],
-                    in0=x_nat[:, :, 0:1].to_broadcast([P, NT, 7]),
+                    in0=first.to_broadcast([P, NT, 7]),
                     in1=bins[:].unsqueeze(1).to_broadcast([P, NT, 7]),
                     op=ALU.is_gt,
                 )
@@ -138,6 +248,10 @@ def tile_dispatchbyvariable_pa_kernel(tc, x, W_bytes, W_scale, out):
             elif k == 2:
                 nc.vector.scalar_tensor_tensor(
                     out=grp[:], in0=cmp[:, :, 3], scalar=-4.0, in1=msum[:], op0=ALU.mult, op1=ALU.add
+                )
+            elif eng == "G":
+                nc.gpsimd.tensor_scalar(
+                    out=low[:], in0=cmp[:, :, 3], scalar1=-1.0, scalar2=1.0, op0=ALU.mult, op1=ALU.add
                 )
             else:
                 nc.vector.tensor_scalar(
@@ -151,33 +265,41 @@ def tile_dispatchbyvariable_pa_kernel(tc, x, W_bytes, W_scale, out):
 
         tbank = {}
 
-        def transposes(i):
-            for h in range(2):
-                bank = psum.tile([P, 2, 2, P], F32, name="tb%d_%d" % (i, h), tag="bank%d" % (4 + (2 * i + h) % 4))
-                tbank[(i, h)] = bank
-                for a2 in range(2):
-                    a = 2 * h + a2
-                    for u in range(2):
-                        nc.tensor.transpose(bank[:, a2, u, :], x_re[:, i, u, :], mident[i][:, P * a : P * (a + 1)])
+        def transposes(i, h):
+            bank = psum.tile([P, 2, 2, P], F32, name="tb%d_%d" % (i, h), tag="bank%d" % trb[(2 * i + h) % len(trb)])
+            tbank[(i, h)] = bank
+            for a2 in range(2):
+                a = 2 * h + a2
+                for u in range(2):
+                    if reorder:
+                        src = x_re[:, i, u, :]
+                    else:
+                        src = x_words[:, 256 * i + u : 256 * (i + 1) : 2]
+                    nc.tensor.transpose(bank[:, a2, u, :], src, mident[i][:, P * a : P * (a + 1)])
 
-        def empty(i):
+        def empty(eng, i, h):
             xm_words = xm[i][:].bitcast(F32)
-            for h in range(2):
-                nc.scalar.copy(
-                    out=xm_words[:, 512 * h : 512 * (h + 1)].rearrange("p (a r u) -> p a r u", a=2, u=2),
-                    in_=tbank[(i, h)][:].rearrange("p a u r -> p a r u"),
-                )
+            dst = xm_words[:, 512 * h : 512 * (h + 1)].rearrange("p (a r u) -> p a r u", a=2, u=2)
+            src = tbank[(i, h)][:].rearrange("p a u r -> p a r u")
+            if eng == "V":
+                nc.vector.tensor_copy(out=dst, in_=src)
+            else:
+                nc.scalar.copy(out=dst, in_=src)
 
         def quantize_x(i):
             nc.vector.quantize_mx(out=xq[i][:].bitcast(FP8X4), scales=xs[i][:], in_=xm[i][:])
 
         acc = {}
+        count = {}
 
         def multiply(e, i):
-            a = e % NG
-            if a == 0:
-                acc_i = psum.tile([P, F], F32, name="acc%d_%d" % (e, i), tag="bank%d" % i)
+            key = (e // NG, i)
+            n = count.get(key, 0)
+            count[key] = n + 1
+            if n == 0:
+                acc_i = psum.tile([P, F], F32, name="acc%d_%d" % key, tag="bank%d" % i)
                 acc[i] = acc_i
+            a = e % NG
             cols = slice(P * a, P * (a + 1))
             nc.tensor.matmul_mx(
                 out=acc[i][:],
@@ -185,17 +307,21 @@ def tile_dispatchbyvariable_pa_kernel(tc, x, W_bytes, W_scale, out):
                 lhsT_scale=xs[i][:, cols],
                 rhs=wq[e][:].bitcast(FP8X4),
                 rhs_scale=ws[e][:],
-                start=(a == 0),
-                stop=(a == NG - 1),
+                start=(n == 0),
+                stop=(n == NG - 1),
             )
 
         part = {}
+        tmp = {}
         out_view = out.rearrange("b t f -> (b t) f").rearrange("(i p) f -> p i f", p=P)
 
-        def keep_low(i):
+        def keep_low(eng, i):
             part_i = keep.tile([P, F], F32, name="part%d" % i)
             part[i] = part_i
-            nc.scalar.activation(out=part_i[:], in_=acc[i][:], func=ACT.Copy, scale=low[:, i : i + 1])
+            if eng == "V":
+                nc.vector.tensor_scalar(out=part_i[:], in0=acc[i][:], scalar1=low[:, i : i + 1], scalar2=None, op0=ALU.mult)
+            else:
+                nc.scalar.activation(out=part_i[:], in_=acc[i][:], func=ACT.Copy, scale=low[:, i : i + 1])
 
         def finish(i):
             res_i = keep.tile([P, F], F32, name="res%d" % i)
@@ -204,68 +330,43 @@ def tile_dispatchbyvariable_pa_kernel(tc, x, W_bytes, W_scale, out):
             )
             nc.sync.dma_start(out=out_view[:, i, :], in_=res_i[:])
 
-        def two_experts(e, skew):
-            for d in range(NT + skew):
-                if d < NT:
-                    multiply(e, d)
-                if 0 <= d - skew:
-                    multiply(e + 1, d - skew)
-                    if e + 1 == NE - 1:
-                        finish(d - skew)
+        def keep_high(i):
+            tmp_i = keep.tile([P, F], F32, name="tmp%d" % i)
+            tmp[i] = tmp_i
+            nc.scalar.activation(out=tmp_i[:], in_=acc[i][:], func=ACT.Copy, scale=cmp[:, i, 3:4])
 
-        widen(0, 0, S)
-        for t in (1, 2, 3):
-            widen(0, t, V)
-        for j in range(NT // 2):
-            reorder(j)
-        interleave_w(0)
-        for k in range(3):
-            bucket(k)
-        widen(1, 0, S)
-        for i in range(NT):
-            mask_identity(i)
-        for i in range(NT):
-            if i == 4:
-                widen(1, 1, S)
-            transposes(i)
-            empty(i)
-        quantize_w(0)
-        interleave_w(1)
-        for i in range(4):
-            quantize_x(i)
-        quantize_w(1)
-        for e in (0, 1):
-            for i in range(4):
-                multiply(e, i)
-        widen(1, 2, V)
-        widen(1, 3, V)
-        interleave_w(2)
-        for i in range(4, NT):
-            quantize_x(i)
-        quantize_w(2)
-        for e in (0, 1):
-            for i in range(4, NT):
-                multiply(e, i)
-        for q, t in ((2, 0), (2, 1), (2, 2), (3, 0), (3, 1)):
-            widen(q, t, S)
-        for i in range(NT):
-            multiply(2, i)
-        interleave_w(3)
-        widen(2, 3, V)
-        bucket(3)
-        quantize_w(3)
-        for i in range(NT):
-            multiply(3, i)
-            keep_low(i)
-        interleave_w(4)
-        widen(3, 2, V)
-        quantize_w(4)
-        interleave_w(5)
-        widen(3, 3, V)
-        quantize_w(5)
-        two_experts(4, 4)
-        interleave_w(6)
-        interleave_w(7)
-        quantize_w(6)
-        quantize_w(7)
-        two_experts(6, 1)
+        def add_parts(i):
+            res_i = keep.tile([P, F], F32, name="res%d" % i)
+            nc.gpsimd.tensor_tensor(out=res_i[:], in0=tmp[i][:], in1=part[i][:], op=ALU.add)
+            nc.sync.dma_start(out=out_view[:, i, :], in_=res_i[:])
+
+        for eng, st in merge(queues, trb, reorder):
+            k = st[0]
+            if k == "wid":
+                widen(eng, st[1], st[2])
+            elif k == "il":
+                interleave_w(eng, st[1])
+            elif k == "qw":
+                quantize_w(st[1])
+            elif k == "reo":
+                reorder_x(st[1])
+            elif k == "buck":
+                bucket(eng, st[1])
+            elif k == "mask":
+                mask_identity(st[1])
+            elif k == "tr":
+                transposes(st[1], st[2])
+            elif k == "emp":
+                empty(eng, st[1], st[2])
+            elif k == "qx":
+                quantize_x(st[1])
+            elif k == "mm":
+                multiply(st[1], st[2])
+            elif k == "low":
+                keep_low(eng, st[1])
+            elif k == "fin":
+                finish(st[1])
+            elif k == "hi":
+                keep_high(st[1])
+            else:
+                add_parts(st[1])

@@ -40,10 +40,10 @@ def plan():
             if d < 8: r.append(('mm', e, d))
             if d >= skew: r.append(('mm', e + 1, d - skew))
         return r
-    P = T('tr', range(6)) + M((0,), range(4)) + T('tr', (6, 7)) + M((1,), range(4)) + M((0, 1), range(4, 8)) + M((2, 3), range(8)) + zipped(4, 5) + zipped(6, 1)
+    P = T('tr', range(5)) + M((0,), (0, 1)) + T('tr', (5,)) + M((0,), (2, 3)) + T('tr', (6,)) + M((1,), (0, 1)) + T('tr', (7,)) + M((1,), (2, 3)) + [('mm', e, i) for i in range(4, 8) for e in (0, 1)] + M((2, 3), range(8)) + zipped(4, 5) + zipped(6, 1)
     QUEUES = {'V': V, 'S': S, 'P': P, 'G': [('buck', 3)]}
     LOADS = [n for n, kib in LOADS]
-    OPT = {"trb": (4, 5, 6, 7), "reorder": False, "pairs2": ()}
+    OPT = {"trb": (4, 5, 6, 7), "reorder": (), "pairs2": (), "uouter": False, "dummy_bank": 3, "small_on_act": False, "last_pieces": 1}
     return LOADS, QUEUES, OPT
 
 
@@ -71,7 +71,7 @@ def needs(st, trb, reorder):
         return [("buck", 2)]
     if k == "tr":
         j = 2 * st[1] + st[2] - len(trb)
-        return [("mask", st[1])] + ([("reo", st[1] // 2)] if reorder else []) + ([("emp", j // 2, j % 2)] if j >= 0 else [])
+        return [("mask", st[1])] + ([("reo", st[1] // 2)] if st[1] // 2 in reorder else []) + [("emp", jj // 2, jj % 2) for jj in (j, j + 1 - st[2]) if jj >= 0]
     if k == "emp":
         return [("tr", st[1], st[2])]
     if k == "qx":
@@ -144,9 +144,9 @@ def tile_dispatchbyvariable_pa_kernel(tc, x, W_bytes, W_scale, out):
         for name in loads:
             if name == "y":
                 use_y = True
-                nc.sync.dma_start(out=yt[:], in_=x_view[:, :, 0:2])
+                (nc.scalar if opt["small_on_act"] else nc.sync).dma_start(out=yt[:], in_=x_view[:, :, 0:2])
             elif name == "wscale":
-                nc.sync.dma_start(out=wscale[:], in_=W_scale.rearrange("o (p t) u -> p (o t u)", t=4))
+                (nc.scalar if opt["small_on_act"] else nc.sync).dma_start(out=wscale[:], in_=W_scale.rearrange("o (p t) u -> p (o t u)", t=4))
             elif name.startswith("w0"):
                 t = int(name[3:])
                 nc.sync.dma_start(out=wbytes[0][:, t, :, :], in_=first_pair[:, t, :, :])
@@ -266,16 +266,29 @@ def tile_dispatchbyvariable_pa_kernel(tc, x, W_bytes, W_scale, out):
         tbank = {}
 
         def transposes(i, h):
-            bank = psum.tile([P, 2, 2, P], F32, name="tb%d_%d" % (i, h), tag="bank%d" % trb[(2 * i + h) % len(trb)])
-            tbank[(i, h)] = bank
-            for a2 in range(2):
-                a = 2 * h + a2
-                for u in range(2):
-                    if reorder:
-                        src = x_re[:, i, u, :]
-                    else:
-                        src = x_words[:, 256 * i + u : 256 * (i + 1) : 2]
-                    nc.tensor.transpose(bank[:, a2, u, :], src, mident[i][:, P * a : P * (a + 1)])
+            if opt["uouter"]:
+                if h == 0:
+                    for hh in range(2):
+                        bank_hh = psum.tile([P, 2, 2, P], F32, name="tb%d_%d" % (i, hh), tag="bank%d" % trb[(2 * i + hh) % len(trb)])
+                        tbank[(i, hh)] = bank_hh
+                    for u in range(2):
+                        if i // 2 in reorder:
+                            src = x_re[:, i, u, :]
+                        else:
+                            src = x_words[:, 256 * i + u : 256 * (i + 1) : 2]
+                        for a in range(NG):
+                            nc.tensor.transpose(tbank[(i, a // 2)][:, a % 2, u, :], src, mident[i][:, P * a : P * (a + 1)])
+            else:
+                bank = psum.tile([P, 2, 2, P], F32, name="tb%d_%d" % (i, h), tag="bank%d" % trb[(2 * i + h) % len(trb)])
+                tbank[(i, h)] = bank
+                for a2 in range(2):
+                    a = 2 * h + a2
+                    for u in range(2):
+                        if i // 2 in reorder:
+                            src = x_re[:, i, u, :]
+                        else:
+                            src = x_words[:, 256 * i + u : 256 * (i + 1) : 2]
+                        nc.tensor.transpose(bank[:, a2, u, :], src, mident[i][:, P * a : P * (a + 1)])
 
         def empty(eng, i, h):
             xm_words = xm[i][:].bitcast(F32)
@@ -325,10 +338,14 @@ def tile_dispatchbyvariable_pa_kernel(tc, x, W_bytes, W_scale, out):
 
         def finish(i):
             res_i = keep.tile([P, F], F32, name="res%d" % i)
-            nc.vector.scalar_tensor_tensor(
-                out=res_i[:], in0=acc[i][:], scalar=cmp[:, i, 3:4], in1=part[i][:], op0=ALU.mult, op1=ALU.add
-            )
-            nc.sync.dma_start(out=out_view[:, i, :], in_=res_i[:])
+            pieces = opt["last_pieces"] if i == NT - 1 else 1
+            width = F // pieces
+            for c in range(pieces):
+                cols = slice(width * c, width * (c + 1))
+                nc.vector.scalar_tensor_tensor(
+                    out=res_i[:, cols], in0=acc[i][:, cols], scalar=cmp[:, i, 3:4], in1=part[i][:, cols], op0=ALU.mult, op1=ALU.add
+                )
+                nc.sync.dma_start(out=out_view[:, i, cols], in_=res_i[:, cols])
 
         def keep_high(i):
             tmp_i = keep.tile([P, F], F32, name="tmp%d" % i)
@@ -339,6 +356,14 @@ def tile_dispatchbyvariable_pa_kernel(tc, x, W_bytes, W_scale, out):
             res_i = keep.tile([P, F], F32, name="res%d" % i)
             nc.gpsimd.tensor_tensor(out=res_i[:], in0=tmp[i][:], in1=part[i][:], op=ALU.add)
             nc.sync.dma_start(out=out_view[:, i, :], in_=res_i[:])
+
+        warm_ops = keep.tile([P, F], BF16, name="warm_ops")
+        if any(st[0] == "dum" for st in queues["P"]):
+            nc.gpsimd.memset(warm_ops[:], 0.0)
+
+        def dummy(n):
+            dummy_n = psum.tile([P, F], F32, name="dummy%d" % n, tag="bank%d" % opt["dummy_bank"])
+            nc.tensor.matmul(out=dummy_n[:], lhsT=warm_ops[:, 0:P], rhs=warm_ops[:], start=True, stop=True)
 
         for eng, st in merge(queues, trb, reorder):
             k = st[0]
@@ -368,5 +393,7 @@ def tile_dispatchbyvariable_pa_kernel(tc, x, W_bytes, W_scale, out):
                 finish(st[1])
             elif k == "hi":
                 keep_high(st[1])
+            elif k == "dum":
+                dummy(st[1])
             else:
                 add_parts(st[1])

@@ -30,9 +30,9 @@ def plan():
     def T(k, l): return [(k, i) for i in l]
     def M(es, tiles): return [('mm', e, i) for e in es for i in tiles]
     V = T('buck', (0, 1, 2)) + T('mask', range(4)) + [('wid', 0, 1), ('wid', 0, 2), ('wid', 0, 3), ('il', 0)] + T('mask', range(4, 8))
-    V += [('qx', 0), ('qx', 1), ('qw', 0), ('il', 1), ('qx', 2), ('qx', 3), ('qw', 1), ('wid', 1, 2), ('wid', 1, 3), ('qx', 4), ('qx', 5), ('il', 2), ('qx', 6), ('qx', 7), ('qw', 2), ('il', 3), ('wid', 2, 3), ('qw', 3)]
+    V += [('qx', 0), ('qx', 1), ('qw', 0), ('il', 1), ('qx', 2), ('qx', 3), ('qw', 1), ('wid', 1, 3), ('qx', 4), ('qx', 5), ('il', 2), ('qx', 6), ('qx', 7), ('qw', 2), ('il', 3), ('wid', 2, 3), ('qw', 3)]
     V += [('il', 4), ('wid', 3, 2), ('qw', 4), ('il', 5), ('wid', 3, 3), ('qw', 5), ('il', 6), ('il', 7), ('qw', 6), ('qw', 7)] + T('fin', range(8))
-    S = [('wid', 0, 0), ('emp', 0), ('emp', 1), ('wid', 1, 0), ('emp', 2), ('emp', 3), ('wid', 1, 1)] + T('emp', range(4, 8))
+    S = [('wid', 0, 0), ('emp', 0), ('emp', 1), ('wid', 1, 0), ('emp', 2), ('emp', 3), ('wid', 1, 1), ('emp', 4), ('wid', 1, 2)] + T('emp', range(5, 8))
     S += [('wid', 2, 0), ('wid', 2, 1), ('wid', 2, 2), ('wid', 3, 0), ('wid', 3, 1)] + T('low', range(8))
     def zipped(e, skew):
         r = []

@@ -14,386 +14,345 @@ ACT = mybir.ActivationFunctionType
 AX = mybir.AxisListType
 
 P = 128
-TOK = 1024
+TOKENS = 1024
 D = 512
 F = 512
-NE = 8
-NT = TOK // P
-NG = 4
-BINS = (-1.5, -1.0, -0.5, 0.0, 0.5, 1.0, 1.5)
+EXPERTS = 8
+TILES = TOKENS // P
+GROUPS = 4
+PACK = 4
+PAIRS = EXPERTS // 2
+TOKEN_WORDS = D // 2
+HALF_WORDS = 2 * P * 2
+BOUNDARIES = (-1.5, -1.0, -0.5, 0.0, 0.5, 1.0, 1.5)
+ZERO_BOUNDARY = 3
+TRANSPOSE_BANKS = (4, 5, 6, 7)
 
-FLOPS = 2 * TOK * D * F * NE
+FLOPS = 2 * TOKENS * D * F * EXPERTS
 
-
-def plan():
-    LOADS = [('y', 16), ('x0', 256), ('wscale', 2)] + [('w0_%d' % t, 128) for t in range(4)] + [('x1', 256), ('we2', 256), ('we3', 256), ('x2', 256), ('we4', 256), ('we5', 256), ('x3', 256), ('we6', 256), ('we7', 256)]
-    def T(k, l): return [(k, i) for i in l]
-    def M(es, tiles): return [('mm', e, i) for e in es for i in tiles]
-    V = T('buck', (0, 1, 2)) + T('mask', range(4)) + [('wid', 0, 1), ('wid', 0, 2), ('wid', 0, 3), ('il', 0)] + T('mask', range(4, 8))
-    V += [('qx', 0), ('qx', 1), ('qw', 0), ('il', 1), ('qx', 2), ('qx', 3), ('qw', 1), ('wid', 1, 3), ('qx', 4), ('qx', 5), ('il', 2), ('qx', 6), ('qx', 7), ('qw', 2), ('il', 3), ('wid', 2, 3), ('qw', 3)]
-    V += [('il', 4), ('wid', 3, 2), ('qw', 4), ('il', 5), ('wid', 3, 3), ('qw', 5), ('il', 6), ('il', 7), ('qw', 6), ('qw', 7)] + T('fin', range(8))
-    S = [('wid', 0, 0), ('emp', 0), ('emp', 1), ('wid', 1, 0), ('emp', 2), ('emp', 3), ('wid', 1, 1), ('emp', 4), ('wid', 1, 2)] + T('emp', range(5, 8))
-    S += [('wid', 2, 0), ('wid', 2, 1), ('wid', 2, 2), ('wid', 3, 0), ('wid', 3, 1)] + T('low', range(8))
-    def zipped(e, skew):
-        r = []
-        for d in range(8 + skew):
-            if d < 8: r.append(('mm', e, d))
-            if d >= skew: r.append(('mm', e + 1, d - skew))
-        return r
-    P = T('tr', range(5)) + M((0,), (0, 1)) + T('tr', (5,)) + M((0,), (2, 3)) + T('tr', (6,)) + M((1,), (0, 1)) + T('tr', (7,)) + M((1,), (2, 3)) + [('mm', e, i) for i in range(4, 8) for e in (0, 1)] + M((2, 3), range(8)) + zipped(4, 5) + zipped(6, 1)
-    QUEUES = {'V': V, 'S': S, 'P': P, 'G': [('buck', 3)]}
-    LOADS = [n for n, kib in LOADS]
-    OPT = {"trb": (4, 5, 6, 7), "reorder": (), "pairs2": (), "uouter": False, "dummy_bank": 3, "small_on_act": False, "last_pieces": 1}
-    return LOADS, QUEUES, OPT
+VECTOR = "vector"
+SCALAR = "scalar"
+TENSOR = "tensor"
+GPSIMD = "gpsimd"
 
 
-def halves(queues):
-    out = {}
-    for eng in queues:
-        out[eng] = []
-        for st in queues[eng]:
-            if st[0] in ("tr", "emp") and len(st) == 2:
-                out[eng].extend([(st[0], st[1], 0), (st[0], st[1], 1)])
-            else:
-                out[eng].append(st)
-    return out
+def steps(kind, numbers):
+    return [(kind, n) for n in numbers]
 
 
-def needs(st, trb, reorder):
-    k = st[0]
-    if k == "il":
-        return [("wid", st[1] // 2, t) for t in range(4)]
-    if k == "qw":
-        return [("il", st[1])]
-    if k == "buck":
-        return [] if st[1] == 0 else [("buck", 0)] if st[1] in (1, 3) else [("buck", 1)]
-    if k == "mask":
-        return [("buck", 2)]
-    if k == "tr":
-        j = 2 * st[1] + st[2] - len(trb)
-        return [("mask", st[1])] + ([("reo", st[1] // 2)] if st[1] // 2 in reorder else []) + [("emp", jj // 2, jj % 2) for jj in (j, j + 1 - st[2]) if jj >= 0]
-    if k == "emp":
-        return [("tr", st[1], st[2])]
-    if k == "qx":
-        return [("emp", st[1], 0), ("emp", st[1], 1)]
-    if k == "mm":
-        r = [("qx", st[2]), ("qw", st[1])]
-        if st[1] < 4 and st[2] in trb:
-            r.extend([("emp", j // 2, j % 2) for j in range(16) if trb[j % len(trb)] == st[2]][-1:])
-        if st[1] >= 4:
-            r.append(("low", st[2]))
-        return r
-    if k == "low":
-        return [("mm", e, st[1]) for e in range(4)] + [("buck", 3)]
-    if k == "fin":
-        return [("mm", e, st[1]) for e in range(4, 8)] + [("low", st[1])]
-    if k == "hi":
-        return [("mm", e, st[1]) for e in range(4, 8)]
-    if k == "add":
-        return [("hi", st[1]), ("low", st[1])]
+def both_halves(kind, tiles):
+    return [(kind, i, h) for i in tiles for h in range(2)]
+
+
+def passes(experts, tiles):
+    return [("multiply", e, i) for e in experts for i in tiles]
+
+
+def in_turn(e, skew):
+    order = []
+    for d in range(TILES + skew):
+        if d < TILES:
+            order.append(("multiply", e, d))
+        if d >= skew:
+            order.append(("multiply", e + 1, d - skew))
+    return order
+
+
+def engine_queues():
+    vector = steps("bucket", range(3)) + steps("mask", range(4))
+    vector += [("widen", 0, 1), ("widen", 0, 2), ("widen", 0, 3), ("interleave", 0)] + steps("mask", range(4, TILES))
+    vector += [("quantize_x", 0), ("quantize_x", 1), ("quantize_w", 0)]
+    vector += [("interleave", 1), ("quantize_x", 2), ("quantize_x", 3), ("quantize_w", 1)]
+    vector += [("widen", 1, 3), ("quantize_x", 4), ("quantize_x", 5)]
+    vector += [("interleave", 2), ("quantize_x", 6), ("quantize_x", 7), ("quantize_w", 2)]
+    vector += [("interleave", 3), ("widen", 2, 3), ("quantize_w", 3)]
+    vector += [("interleave", 4), ("widen", 3, 2), ("quantize_w", 4)]
+    vector += [("interleave", 5), ("widen", 3, 3), ("quantize_w", 5)]
+    vector += [("interleave", 6), ("interleave", 7), ("quantize_w", 6), ("quantize_w", 7)]
+    vector += steps("finish", range(TILES))
+
+    scalar = [("widen", 0, 0)] + both_halves("empty", (0, 1))
+    scalar += [("widen", 1, 0)] + both_halves("empty", (2, 3))
+    scalar += [("widen", 1, 1)] + both_halves("empty", (4,))
+    scalar += [("widen", 1, 2)] + both_halves("empty", (5, 6, 7))
+    scalar += [("widen", 2, 0), ("widen", 2, 1), ("widen", 2, 2), ("widen", 3, 0), ("widen", 3, 1)]
+    scalar += steps("keep_low", range(TILES))
+
+    tensor = both_halves("transpose", range(5)) + passes((0,), (0, 1))
+    tensor += both_halves("transpose", (5,)) + passes((0,), (2, 3))
+    tensor += both_halves("transpose", (6,)) + passes((1,), (0, 1))
+    tensor += both_halves("transpose", (7,)) + passes((1,), (2, 3))
+    tensor += [("multiply", e, i) for i in range(4, TILES) for e in (0, 1)]
+    tensor += passes((2, 3), range(TILES))
+    tensor += in_turn(4, 5) + in_turn(6, 1)
+
+    return {VECTOR: vector, SCALAR: scalar, TENSOR: tensor, GPSIMD: [("bucket", 3)]}
+
+
+def needs(step):
+    kind = step[0]
+    if kind == "interleave":
+        return [("widen", step[1] // 2, t) for t in range(PACK)]
+    if kind == "quantize_w":
+        return [("interleave", step[1])]
+    if kind == "bucket":
+        return [] if step[1] == 0 else [("bucket", 0)] if step[1] in (1, 3) else [("bucket", 1)]
+    if kind == "mask":
+        return [("bucket", 2)]
+    if kind == "transpose":
+        before = 2 * step[1] + step[2] - len(TRANSPOSE_BANKS)
+        return [("mask", step[1])] + [("empty", b // 2, b % 2) for b in (before, before + 1 - step[2]) if b >= 0]
+    if kind == "empty":
+        return [("transpose", step[1], step[2])]
+    if kind == "quantize_x":
+        return [("empty", step[1], 0), ("empty", step[1], 1)]
+    if kind == "multiply":
+        e, i = step[1], step[2]
+        before = [("quantize_x", i), ("quantize_w", e)]
+        if e < GROUPS and i in TRANSPOSE_BANKS:
+            last = [b for b in range(2 * TILES) if TRANSPOSE_BANKS[b % len(TRANSPOSE_BANKS)] == i][-1]
+            before.append(("empty", last // 2, last % 2))
+        if e >= GROUPS:
+            before.append(("keep_low", i))
+        return before
+    if kind == "keep_low":
+        return [("multiply", e, step[1]) for e in range(GROUPS)] + [("bucket", 3)]
+    if kind == "finish":
+        return [("multiply", e, step[1]) for e in range(GROUPS, EXPERTS)] + [("keep_low", step[1])]
     return []
 
 
-def merge(queues, trb, reorder):
-    pos = {}
-    for eng in queues:
-        pos[eng] = 0
-    emitted = set()
+def text_order(queues):
+    position = {}
+    for engine in queues:
+        position[engine] = 0
+    written = set()
     text = []
-    for rounds in range(10000):
-        moved = False
-        for eng in queues:
-            for tries in range(len(queues[eng])):
-                if pos[eng] >= len(queues[eng]):
+    total = sum(len(queues[engine]) for engine in queues)
+    for rounds in range(total):
+        for engine in queues:
+            for tries in range(len(queues[engine])):
+                if position[engine] >= len(queues[engine]):
                     break
-                st = queues[eng][pos[eng]]
-                if not all(n in emitted for n in needs(st, trb, reorder)):
+                step = queues[engine][position[engine]]
+                if not all(n in written for n in needs(step)):
                     break
-                text.append((eng, st))
-                emitted.add(st)
-                pos[eng] = pos[eng] + 1
-                moved = True
-        if not moved:
-            break
-    assert all(pos[eng] == len(queues[eng]) for eng in queues), "the queues block each other"
+                text.append((engine, step))
+                written.add(step)
+                position[engine] = position[engine] + 1
+    assert len(text) == total, "the queues block each other"
     return text
 
 
 def tile_dispatchbyvariable_pa_kernel(tc, x, W_bytes, W_scale, out):
     nc = tc.nc
-    loads, queues, opt = plan()
-    queues = halves(queues)
-    trb = opt["trb"]
-    reorder = opt["reorder"]
-    pairs2 = opt["pairs2"]
     with ExitStack() as ctx:
         keep = ctx.enter_context(tc.tile_pool(name="keep", bufs=1))
         psum = ctx.enter_context(tc.psum_pool(name="psum", bufs=1))
         ctx.enter_context(tc.manual_schedule())
 
-        wscale = keep.tile([P, 4], F32, name="wscale")
-        wbytes = []
-        for q in range(NE // 2):
-            wbytes_q = keep.tile([P, 4, 2, F], U8, name="wbytes%d" % q)
-            wbytes.append(wbytes_q)
-        x_nat = keep.tile([P, NT, D], BF16, name="x_nat")
+        w_scale = keep.tile([P, PACK], F32, name="w_scale")
+        w_bytes = []
+        for q in range(PAIRS):
+            w_bytes_q = keep.tile([P, PACK, 2, F], U8, name="w_bytes%d" % q)
+            w_bytes.append(w_bytes_q)
+        x_rows = keep.tile([P, TILES, D], BF16, name="x_rows")
         x_view = x.rearrange("b t d -> (b t) d").rearrange("(i p) d -> p i d", p=P)
-        yt = keep.tile([P, NT, 2], BF16, name="yt")
-        first_pair = W_bytes[0:2].rearrange("e (p t) n -> p t e n", t=4)
-        use_y = False
-        for name in loads:
-            if name == "y":
-                use_y = True
-                (nc.scalar if opt["small_on_act"] else nc.sync).dma_start(out=yt[:], in_=x_view[:, :, 0:2])
-            elif name == "wscale":
-                (nc.scalar if opt["small_on_act"] else nc.sync).dma_start(out=wscale[:], in_=W_scale.rearrange("o (p t) u -> p (o t u)", t=4))
-            elif name.startswith("w0"):
-                t = int(name[3:])
-                nc.sync.dma_start(out=wbytes[0][:, t, :, :], in_=first_pair[:, t, :, :])
-            elif name.startswith("we"):
-                e = int(name[2:])
-                nc.sync.dma_start(out=wbytes[e // 2][:, :, e % 2, :], in_=W_bytes[e].rearrange("(p t) n -> p t n", t=4))
-            else:
-                j = int(name[1:])
-                nc.sync.dma_start(out=x_nat[:, 2 * j : 2 * j + 2, :], in_=x_view[:, 2 * j : 2 * j + 2, :])
+        feature = keep.tile([P, TILES, 2], BF16, name="feature")
 
-        col_minus_row = keep.tile([P, NG * P], I32, name="col_minus_row")
-        nc.gpsimd.iota(col_minus_row[:], pattern=[[1, NG * P]], base=0, channel_multiplier=-1)
-        bins = keep.tile([P, 7], F32, name="bins")
-        for j in range(7):
-            nc.vector.memset(bins[:, j : j + 1], BINS[j])
-        warm = keep.tile([P, 1], F32, name="warm")
-        nc.scalar.activation(out=warm[:], in_=bins[:, 0:1], func=ACT.Copy)
-        block_of_col = keep.tile([P, NG * P], F32, name="block_of_col")
-        nc.vector.tensor_scalar(out=block_of_col[:], in0=col_minus_row[:], scalar1=1.0 / P, scalar2=None, op0=ALU.mult)
+        def load_x(j):
+            nc.sync.dma_start(out=x_rows[:, 2 * j : 2 * j + 2, :], in_=x_view[:, 2 * j : 2 * j + 2, :])
 
-        wplanes = []
-        for q in range(NE // 2):
-            wplanes_q = keep.tile([P, 4 * 2 * F], BF16, name="wplanes%d" % q)
-            wplanes.append(wplanes_q)
-        wil = []
-        wq = []
-        ws = []
-        for e in range(NE):
-            wil_e = keep.tile([P, 4 * F], BF16, name="wil%d" % e, align_bytes=64)
-            wq_e = keep.tile([P, F], U32, name="wq%d" % e, align_bytes=64)
-            ws_e = keep.tile([P, F], U8, name="ws%d" % e, align_bytes=64)
-            wil.append(wil_e)
-            wq.append(wq_e)
-            ws.append(ws_e)
-
-        def widen(eng, q, t):
-            src = wbytes[q][:, t, :, :].rearrange("p e n -> p (e n)").bitcast(FP8)
-            if q in pairs2:
-                dst = wplanes[q][:].rearrange("p (u m v) -> p u m v", u=2, v=2)[:, t // 2, :, t % 2]
-            else:
-                dst = wplanes[q][:].rearrange("p (t m) -> p t m", t=4)[:, t, :]
-            if eng == "V":
-                nc.vector.tensor_scalar(out=dst, in0=src, scalar1=wscale[:, t : t + 1], scalar2=None, op0=ALU.mult)
-            else:
-                nc.scalar.activation(out=dst, in_=src, func=ACT.Copy, scale=wscale[:, t : t + 1])
-
-        def interleave_w(eng, e):
-            if e // 2 in pairs2:
-                dst = wil[e][:].bitcast(F32).rearrange("p (n u) -> p n u", u=2)
-                src = wplanes[e // 2][:].bitcast(F32).rearrange("p (u e n) -> p u e n", u=2, e=2)[:, :, e % 2, :].rearrange("p u n -> p n u")
-            else:
-                dst = wil[e][:].rearrange("p (n t) -> p n t", t=4)
-                src = wplanes[e // 2][:].rearrange("p (t e n) -> p t e n", t=4, e=2)[:, :, e % 2, :].rearrange("p t n -> p n t")
-            if eng == "V":
-                nc.vector.tensor_copy(out=dst, in_=src)
-            else:
-                nc.scalar.copy(out=dst, in_=src)
-
-        def quantize_w(e):
-            nc.vector.quantize_mx(out=wq[e][:].bitcast(FP8X4), scales=ws[e][:], in_=wil[e][:])
-
-        cmp = keep.tile([P, NT, 7], F32, name="cmp")
-        msum = keep.tile([P, NT], F32, name="msum")
-        grp = keep.tile([P, NT], F32, name="grp")
-        low = keep.tile([P, NT], F32, name="low")
-        x_re = keep.tile([P, NT, 2, P], F32, name="x_re")
-        mident = []
-        xm = []
-        xq = []
-        xs = []
-        for i in range(NT):
-            mident_i = keep.tile([P, NG * P], F32, name="mident%d" % i)
-            xm_i = keep.tile([P, NG * P * 4], BF16, name="xm%d" % i, align_bytes=64)
-            xq_i = keep.tile([P, NG * P], U32, name="xq%d" % i, align_bytes=64)
-            xs_i = keep.tile([P, NG * P], U8, name="xs%d" % i, align_bytes=64)
-            mident.append(mident_i)
-            xm.append(xm_i)
-            xq.append(xq_i)
-            xs.append(xs_i)
-        x_words = x_nat[:].rearrange("p i d -> p (i d)").bitcast(F32)
-
-        def reorder_x(j):
-            nc.scalar.copy(
-                out=x_re[:, 2 * j : 2 * j + 2, :, :],
-                in_=x_words[:, 512 * j : 512 * (j + 1)].rearrange("p (i w u) -> p i u w", i=2, u=2),
+        def load_w(e):
+            nc.sync.dma_start(
+                out=w_bytes[e // 2][:, :, e % 2, :], in_=W_bytes[e].rearrange("(p t) n -> p t n", t=PACK)
             )
 
-        def bucket(eng, k):
+        nc.sync.dma_start(out=feature[:], in_=x_view[:, :, 0:2])
+        load_x(0)
+        nc.sync.dma_start(out=w_scale[:], in_=W_scale.rearrange("o (p t) u -> p (o t u)", t=PACK))
+        first_pair = W_bytes[0:2].rearrange("e (p t) n -> p t e n", t=PACK)
+        for t in range(PACK):
+            nc.sync.dma_start(out=w_bytes[0][:, t, :, :], in_=first_pair[:, t, :, :])
+        for j in range(1, TILES // 2):
+            load_x(j)
+            load_w(2 * j)
+            load_w(2 * j + 1)
+
+        col_minus_row = keep.tile([P, GROUPS * P], I32, name="col_minus_row")
+        nc.gpsimd.iota(col_minus_row[:], pattern=[[1, GROUPS * P]], base=0, channel_multiplier=-1)
+        boundaries = keep.tile([P, len(BOUNDARIES)], F32, name="boundaries")
+        for j in range(len(BOUNDARIES)):
+            nc.vector.memset(boundaries[:, j : j + 1], BOUNDARIES[j])
+        table_load = keep.tile([P, 1], F32, name="table_load")
+        nc.scalar.activation(out=table_load[:], in_=boundaries[:, 0:1], func=ACT.Copy)
+        block_of_col = keep.tile([P, GROUPS * P], F32, name="block_of_col")
+        nc.vector.tensor_scalar(out=block_of_col[:], in0=col_minus_row[:], scalar1=1.0 / P, scalar2=None, op0=ALU.mult)
+
+        w_planes = []
+        for q in range(PAIRS):
+            w_planes_q = keep.tile([P, PACK, 2, F], BF16, name="w_planes%d" % q)
+            w_planes.append(w_planes_q)
+        w_grouped = []
+        w_codes = []
+        w_scales = []
+        for e in range(EXPERTS):
+            w_grouped_e = keep.tile([P, PACK * F], BF16, name="w_grouped%d" % e, align_bytes=64)
+            w_codes_e = keep.tile([P, F], U32, name="w_codes%d" % e, align_bytes=64)
+            w_scales_e = keep.tile([P, F], U8, name="w_scales%d" % e, align_bytes=64)
+            w_grouped.append(w_grouped_e)
+            w_codes.append(w_codes_e)
+            w_scales.append(w_scales_e)
+
+        def widen(engine, q, t):
+            codes = w_bytes[q][:, t, :, :].rearrange("p e n -> p (e n)").bitcast(FP8)
+            values = w_planes[q][:, t, :, :].rearrange("p e n -> p (e n)")
+            if engine == VECTOR:
+                nc.vector.tensor_scalar(out=values, in0=codes, scalar1=w_scale[:, t : t + 1], scalar2=None, op0=ALU.mult)
+            else:
+                nc.scalar.activation(out=values, in_=codes, func=ACT.Copy, scale=w_scale[:, t : t + 1])
+
+        def interleave(e):
+            nc.vector.tensor_copy(
+                out=w_grouped[e][:].rearrange("p (n t) -> p n t", t=PACK),
+                in_=w_planes[e // 2][:, :, e % 2, :].rearrange("p t n -> p n t"),
+            )
+
+        def quantize_w(e):
+            nc.vector.quantize_mx(out=w_codes[e][:].bitcast(FP8X4), scales=w_scales[e][:], in_=w_grouped[e][:])
+
+        above = keep.tile([P, TILES, len(BOUNDARIES)], F32, name="above")
+        m_count = keep.tile([P, TILES], F32, name="m_count")
+        group = keep.tile([P, TILES], F32, name="group")
+        low = keep.tile([P, TILES], F32, name="low")
+        masked_identity = []
+        x_grouped = []
+        x_codes = []
+        x_scales = []
+        for i in range(TILES):
+            masked_identity_i = keep.tile([P, GROUPS * P], F32, name="masked_identity%d" % i)
+            x_grouped_i = keep.tile([P, GROUPS * P * PACK], BF16, name="x_grouped%d" % i, align_bytes=64)
+            x_codes_i = keep.tile([P, GROUPS * P], U32, name="x_codes%d" % i, align_bytes=64)
+            x_scales_i = keep.tile([P, GROUPS * P], U8, name="x_scales%d" % i, align_bytes=64)
+            masked_identity.append(masked_identity_i)
+            x_grouped.append(x_grouped_i)
+            x_codes.append(x_codes_i)
+            x_scales.append(x_scales_i)
+        x_words = x_rows[:].rearrange("p i d -> p (i d)").bitcast(F32)
+        high = above[:, :, ZERO_BOUNDARY]
+
+        def bucket(k):
             if k == 0:
-                first = yt[:, :, 0:1] if use_y else x_nat[:, :, 0:1]
                 nc.vector.tensor_tensor(
-                    out=cmp[:],
-                    in0=first.to_broadcast([P, NT, 7]),
-                    in1=bins[:].unsqueeze(1).to_broadcast([P, NT, 7]),
+                    out=above[:],
+                    in0=feature[:, :, 0:1].to_broadcast([P, TILES, len(BOUNDARIES)]),
+                    in1=boundaries[:].unsqueeze(1).to_broadcast([P, TILES, len(BOUNDARIES)]),
                     op=ALU.is_gt,
                 )
             elif k == 1:
-                nc.vector.tensor_reduce(out=msum[:], in_=cmp[:], axis=AX.X, op=ALU.add)
+                nc.vector.tensor_reduce(out=m_count[:], in_=above[:], axis=AX.X, op=ALU.add)
             elif k == 2:
                 nc.vector.scalar_tensor_tensor(
-                    out=grp[:], in0=cmp[:, :, 3], scalar=-4.0, in1=msum[:], op0=ALU.mult, op1=ALU.add
-                )
-            elif eng == "G":
-                nc.gpsimd.tensor_scalar(
-                    out=low[:], in0=cmp[:, :, 3], scalar1=-1.0, scalar2=1.0, op0=ALU.mult, op1=ALU.add
+                    out=group[:], in0=high, scalar=-float(GROUPS), in1=m_count[:], op0=ALU.mult, op1=ALU.add
                 )
             else:
-                nc.vector.tensor_scalar(
-                    out=low[:], in0=cmp[:, :, 3], scalar1=-1.0, scalar2=1.0, op0=ALU.mult, op1=ALU.add
-                )
+                nc.gpsimd.tensor_scalar(out=low[:], in0=high, scalar1=-1.0, scalar2=1.0, op0=ALU.mult, op1=ALU.add)
 
-        def mask_identity(i):
+        def mask(i):
             nc.vector.tensor_scalar(
-                out=mident[i][:], in0=block_of_col[:], scalar1=grp[:, i : i + 1], scalar2=None, op0=ALU.is_equal
+                out=masked_identity[i][:], in0=block_of_col[:], scalar1=group[:, i : i + 1], scalar2=None, op0=ALU.is_equal
             )
 
-        tbank = {}
+        turned = {}
 
-        def transposes(i, h):
-            if opt["uouter"]:
-                if h == 0:
-                    for hh in range(2):
-                        bank_hh = psum.tile([P, 2, 2, P], F32, name="tb%d_%d" % (i, hh), tag="bank%d" % trb[(2 * i + hh) % len(trb)])
-                        tbank[(i, hh)] = bank_hh
-                    for u in range(2):
-                        if i // 2 in reorder:
-                            src = x_re[:, i, u, :]
-                        else:
-                            src = x_words[:, 256 * i + u : 256 * (i + 1) : 2]
-                        for a in range(NG):
-                            nc.tensor.transpose(tbank[(i, a // 2)][:, a % 2, u, :], src, mident[i][:, P * a : P * (a + 1)])
-            else:
-                bank = psum.tile([P, 2, 2, P], F32, name="tb%d_%d" % (i, h), tag="bank%d" % trb[(2 * i + h) % len(trb)])
-                tbank[(i, h)] = bank
-                for a2 in range(2):
-                    a = 2 * h + a2
-                    for u in range(2):
-                        if i // 2 in reorder:
-                            src = x_re[:, i, u, :]
-                        else:
-                            src = x_words[:, 256 * i + u : 256 * (i + 1) : 2]
-                        nc.tensor.transpose(bank[:, a2, u, :], src, mident[i][:, P * a : P * (a + 1)])
+        def transpose(i, h):
+            bank = psum.tile(
+                [P, 2, 2, P],
+                F32,
+                name="turned%d_%d" % (i, h),
+                tag="bank%d" % TRANSPOSE_BANKS[(2 * i + h) % len(TRANSPOSE_BANKS)],
+            )
+            turned[(i, h)] = bank
+            for a in (2 * h, 2 * h + 1):
+                for u in range(2):
+                    nc.tensor.transpose(
+                        bank[:, a - 2 * h, u, :],
+                        x_words[:, TOKEN_WORDS * i + u : TOKEN_WORDS * (i + 1) : 2],
+                        masked_identity[i][:, P * a : P * (a + 1)],
+                    )
 
-        def empty(eng, i, h):
-            xm_words = xm[i][:].bitcast(F32)
-            dst = xm_words[:, 512 * h : 512 * (h + 1)].rearrange("p (a r u) -> p a r u", a=2, u=2)
-            src = tbank[(i, h)][:].rearrange("p a u r -> p a r u")
-            if eng == "V":
-                nc.vector.tensor_copy(out=dst, in_=src)
-            else:
-                nc.scalar.copy(out=dst, in_=src)
+        def empty(i, h):
+            words = x_grouped[i][:].bitcast(F32)
+            nc.scalar.copy(
+                out=words[:, HALF_WORDS * h : HALF_WORDS * (h + 1)].rearrange("p (a r u) -> p a r u", a=2, u=2),
+                in_=turned[(i, h)][:].rearrange("p a u r -> p a r u"),
+            )
 
         def quantize_x(i):
-            nc.vector.quantize_mx(out=xq[i][:].bitcast(FP8X4), scales=xs[i][:], in_=xm[i][:])
+            nc.vector.quantize_mx(out=x_codes[i][:].bitcast(FP8X4), scales=x_scales[i][:], in_=x_grouped[i][:])
 
-        acc = {}
-        count = {}
+        sums = {}
+        done = {}
 
         def multiply(e, i):
-            key = (e // NG, i)
-            n = count.get(key, 0)
-            count[key] = n + 1
+            sweep = e // GROUPS
+            n = done.get((sweep, i), 0)
+            done[(sweep, i)] = n + 1
             if n == 0:
-                acc_i = psum.tile([P, F], F32, name="acc%d_%d" % key, tag="bank%d" % i)
-                acc[i] = acc_i
-            a = e % NG
-            cols = slice(P * a, P * (a + 1))
+                sums_i = psum.tile([P, F], F32, name="sums%d_%d" % (sweep, i), tag="bank%d" % i)
+                sums[i] = sums_i
+            cols = slice(P * (e % GROUPS), P * (e % GROUPS + 1))
             nc.tensor.matmul_mx(
-                out=acc[i][:],
-                lhsT=xq[i][:, cols].bitcast(FP8X4),
-                lhsT_scale=xs[i][:, cols],
-                rhs=wq[e][:].bitcast(FP8X4),
-                rhs_scale=ws[e][:],
+                out=sums[i][:],
+                lhsT=x_codes[i][:, cols].bitcast(FP8X4),
+                lhsT_scale=x_scales[i][:, cols],
+                rhs=w_codes[e][:].bitcast(FP8X4),
+                rhs_scale=w_scales[e][:],
                 start=(n == 0),
-                stop=(n == NG - 1),
+                stop=(n == GROUPS - 1),
             )
 
-        part = {}
-        tmp = {}
+        low_part = {}
         out_view = out.rearrange("b t f -> (b t) f").rearrange("(i p) f -> p i f", p=P)
 
-        def keep_low(eng, i):
-            part_i = keep.tile([P, F], F32, name="part%d" % i)
-            part[i] = part_i
-            if eng == "V":
-                nc.vector.tensor_scalar(out=part_i[:], in0=acc[i][:], scalar1=low[:, i : i + 1], scalar2=None, op0=ALU.mult)
-            else:
-                nc.scalar.activation(out=part_i[:], in_=acc[i][:], func=ACT.Copy, scale=low[:, i : i + 1])
+        def keep_low(i):
+            low_part_i = keep.tile([P, F], F32, name="low_part%d" % i)
+            low_part[i] = low_part_i
+            nc.scalar.activation(out=low_part_i[:], in_=sums[i][:], func=ACT.Copy, scale=low[:, i : i + 1])
 
         def finish(i):
-            res_i = keep.tile([P, F], F32, name="res%d" % i)
-            pieces = opt["last_pieces"] if i == NT - 1 else 1
-            width = F // pieces
-            for c in range(pieces):
-                cols = slice(width * c, width * (c + 1))
-                nc.vector.scalar_tensor_tensor(
-                    out=res_i[:, cols], in0=acc[i][:, cols], scalar=cmp[:, i, 3:4], in1=part[i][:, cols], op0=ALU.mult, op1=ALU.add
-                )
-                nc.sync.dma_start(out=out_view[:, i, cols], in_=res_i[:, cols])
+            result_i = keep.tile([P, F], F32, name="result%d" % i)
+            nc.vector.scalar_tensor_tensor(
+                out=result_i[:],
+                in0=sums[i][:],
+                scalar=above[:, i, ZERO_BOUNDARY : ZERO_BOUNDARY + 1],
+                in1=low_part[i][:],
+                op0=ALU.mult,
+                op1=ALU.add,
+            )
+            nc.sync.dma_start(out=out_view[:, i, :], in_=result_i[:])
 
-        def keep_high(i):
-            tmp_i = keep.tile([P, F], F32, name="tmp%d" % i)
-            tmp[i] = tmp_i
-            nc.scalar.activation(out=tmp_i[:], in_=acc[i][:], func=ACT.Copy, scale=cmp[:, i, 3:4])
-
-        def add_parts(i):
-            res_i = keep.tile([P, F], F32, name="res%d" % i)
-            nc.gpsimd.tensor_tensor(out=res_i[:], in0=tmp[i][:], in1=part[i][:], op=ALU.add)
-            nc.sync.dma_start(out=out_view[:, i, :], in_=res_i[:])
-
-        warm_ops = keep.tile([P, F], BF16, name="warm_ops")
-        if any(st[0] == "dum" for st in queues["P"]):
-            nc.gpsimd.memset(warm_ops[:], 0.0)
-
-        def dummy(n):
-            dummy_n = psum.tile([P, F], F32, name="dummy%d" % n, tag="bank%d" % opt["dummy_bank"])
-            nc.tensor.matmul(out=dummy_n[:], lhsT=warm_ops[:, 0:P], rhs=warm_ops[:], start=True, stop=True)
-
-        for eng, st in merge(queues, trb, reorder):
-            k = st[0]
-            if k == "wid":
-                widen(eng, st[1], st[2])
-            elif k == "il":
-                interleave_w(eng, st[1])
-            elif k == "qw":
-                quantize_w(st[1])
-            elif k == "reo":
-                reorder_x(st[1])
-            elif k == "buck":
-                bucket(eng, st[1])
-            elif k == "mask":
-                mask_identity(st[1])
-            elif k == "tr":
-                transposes(st[1], st[2])
-            elif k == "emp":
-                empty(eng, st[1], st[2])
-            elif k == "qx":
-                quantize_x(st[1])
-            elif k == "mm":
-                multiply(st[1], st[2])
-            elif k == "low":
-                keep_low(eng, st[1])
-            elif k == "fin":
-                finish(st[1])
-            elif k == "hi":
-                keep_high(st[1])
-            elif k == "dum":
-                dummy(st[1])
+        for engine, step in text_order(engine_queues()):
+            kind = step[0]
+            if kind == "widen":
+                widen(engine, step[1], step[2])
+            elif kind == "interleave":
+                interleave(step[1])
+            elif kind == "quantize_w":
+                quantize_w(step[1])
+            elif kind == "bucket":
+                bucket(step[1])
+            elif kind == "mask":
+                mask(step[1])
+            elif kind == "transpose":
+                transpose(step[1], step[2])
+            elif kind == "empty":
+                empty(step[1], step[2])
+            elif kind == "quantize_x":
+                quantize_x(step[1])
+            elif kind == "multiply":
+                multiply(step[1], step[2])
+            elif kind == "keep_low":
+                keep_low(step[1])
             else:
-                add_parts(st[1])
+                finish(step[1])

@@ -59,9 +59,9 @@ def in_turn(e, skew):
 
 
 def engine_queues():
-    vector = steps("bucket", range(3)) + steps("mask", range(4))
-    vector += [("widen", 0, 1), ("widen", 0, 2), ("widen", 0, 3), ("interleave", 0)] + steps("mask", range(4, TILES))
-    vector += [("quantize_x", 0), ("quantize_x", 1), ("quantize_w", 0)]
+    vector = steps("bucket", range(3)) + steps("mask", range(2))
+    vector += [("widen", 0, 1), ("widen", 0, 2), ("widen", 0, 3)] + steps("mask", (2, 3)) + [("interleave", 0)]
+    vector += [("quantize_x", 0), ("quantize_w", 0), ("quantize_x", 1)] + steps("mask", range(4, TILES))
     vector += [("interleave", 1), ("quantize_x", 2), ("quantize_x", 3), ("quantize_w", 1)]
     vector += [("widen", 1, 3), ("quantize_x", 4), ("quantize_x", 5)]
     vector += [("interleave", 2), ("quantize_x", 6), ("quantize_x", 7), ("quantize_w", 2)]
@@ -78,8 +78,8 @@ def engine_queues():
     scalar += [("widen", 2, 0), ("widen", 2, 1), ("widen", 2, 2), ("widen", 3, 0), ("widen", 3, 1)]
     scalar += steps("keep_low", range(TILES))
 
-    tensor = both_halves("transpose", range(5)) + passes((0,), (0, 1))
-    tensor += both_halves("transpose", (5,)) + passes((0,), (2, 3))
+    tensor = both_halves("transpose", range(4)) + passes((0,), (0, 1))
+    tensor += both_halves("transpose", (4, 5)) + passes((0,), (2, 3))
     tensor += both_halves("transpose", (6,)) + passes((1,), (0, 1))
     tensor += both_halves("transpose", (7,)) + passes((1,), (2, 3))
     tensor += [("multiply", e, i) for i in range(4, TILES) for e in (0, 1)]

@@ -26,6 +26,7 @@ TOKEN_WORDS = D // 2
 HALF_WORDS = 2 * P * 2
 BOUNDARIES = (-1.5, -1.0, -0.5, 0.0, 0.5, 1.0, 1.5)
 ZERO_BOUNDARY = 3
+FEATURE_ROW = 16
 TRANSPOSE_BANKS = (4, 5, 6, 7)
 
 FLOPS = 2 * TOKENS * D * F * EXPERTS
@@ -158,7 +159,7 @@ def tile_dispatchbyvariable_pa_kernel(tc, x, W_bytes, W_scale, out):
             w_bytes.append(w_bytes_q)
         x_rows = keep.tile([P, TILES, D], BF16, name="x_rows")
         x_view = x.rearrange("b t d -> (b t) d").rearrange("(i p) d -> p i d", p=P)
-        feature = keep.tile([P, TILES, 2], BF16, name="feature")
+        feature = keep.tile([P, TILES, FEATURE_ROW], BF16, name="feature")
 
         def load_x(j):
             nc.sync.dma_start(out=x_rows[:, 2 * j : 2 * j + 2, :], in_=x_view[:, 2 * j : 2 * j + 2, :])
@@ -168,7 +169,7 @@ def tile_dispatchbyvariable_pa_kernel(tc, x, W_bytes, W_scale, out):
                 out=w_bytes[e // 2][:, :, e % 2, :], in_=W_bytes[e].rearrange("(p t) n -> p t n", t=PACK)
             )
 
-        nc.sync.dma_start(out=feature[:], in_=x_view[:, :, 0:2])
+        nc.sync.dma_start(out=feature[:], in_=x_view[:, :, 0:FEATURE_ROW])
         load_x(0)
         nc.sync.dma_start(out=w_scale[:], in_=W_scale.rearrange("o (p t) u -> p (o t u)", t=PACK))
         first_pair = W_bytes[0:2].rearrange("e (p t) n -> p t e n", t=PACK)

@@ -215,8 +215,8 @@ def tile_dispatchbyvariable_pa_kernel(tc, x, W_bytes, W_scale, out):
 
         def interleave(e):
             nc.vector.tensor_copy(
-                out=w_grouped[e][:].rearrange("p (n t) -> p n t", t=PACK),
-                in_=w_planes[e // 2][:, :, e % 2, :].rearrange("p t n -> p n t"),
+                out=w_grouped[e][:].rearrange("p (c i t) -> p c t i", i=4, t=PACK),
+                in_=w_planes[e // 2][:, :, e % 2, :].rearrange("p t (c i) -> p c t i", i=4),
             )
 
         def quantize_w(e):

@@ -85,7 +85,7 @@ def engine_queues():
     tensor += both_halves("transpose", (7,)) + passes((1,), (2, 3))
     tensor += [("multiply", e, i) for i in range(4, TILES) for e in (0, 1)]
     tensor += passes((2, 3), range(TILES))
-    tensor += in_turn(4, 5) + in_turn(6, 1)
+    tensor += in_turn(4, 4) + in_turn(6, 1)
 
     return {VECTOR: vector, SCALAR: scalar, TENSOR: tensor, GPSIMD: [("bucket", 3)]}
 

from contextlib import ExitStack

import concourse.mybir as mybir

F32 = mybir.dt.float32
BF16 = mybir.dt.bfloat16
I32 = mybir.dt.int32
U32 = mybir.dt.uint32
U8 = mybir.dt.uint8
FP8 = mybir.dt.float8_e4m3fn
FP8X4 = mybir.dt.float8_e4m3fn_x4
ALU = mybir.AluOpType
ACT = mybir.ActivationFunctionType
AX = mybir.AxisListType

P = 128
TOKENS = 1024
D = 512
F = 512
EXPERTS = 8
TILES = TOKENS // P
GROUPS = 4
PACK = 4
PAIRS = EXPERTS // 2
TOKEN_WORDS = D // 2
HALF_WORDS = 2 * P * 2
BOUNDARIES = (-1.5, -1.0, -0.5, 0.0, 0.5, 1.0, 1.5)
ZERO_BOUNDARY = 3
FEATURE_ROW = 16
TRANSPOSE_BANKS = (4, 5, 6, 7)

FLOPS = 2 * TOKENS * D * F * EXPERTS

VECTOR = "vector"
SCALAR = "scalar"
TENSOR = "tensor"
GPSIMD = "gpsimd"


def steps(kind, numbers):
    return [(kind, n) for n in numbers]


def both_halves(kind, tiles):
    return [(kind, i, h) for i in tiles for h in range(2)]


def passes(experts, tiles):
    return [("multiply", e, i) for e in experts for i in tiles]


def in_turn(e, skew):
    order = []
    for d in range(TILES + skew):
        if d < TILES:
            order.append(("multiply", e, d))
        if d >= skew:
            order.append(("multiply", e + 1, d - skew))
    return order


def engine_queues():
    vector = steps("bucket", range(3)) + steps("mask", range(2))
    vector += [("widen", 0, 1), ("widen", 0, 2), ("widen", 0, 3)] + steps("mask", (2, 3)) + [("interleave", 0)]
    vector += [("quantize_x", 0), ("quantize_w", 0), ("quantize_x", 1)] + steps("mask", range(4, TILES))
    vector += [("interleave", 1), ("quantize_x", 2), ("quantize_x", 3), ("quantize_w", 1)]
    vector += [("widen", 1, 3), ("quantize_x", 4), ("quantize_x", 5)]
    vector += [("interleave", 2), ("quantize_x", 6), ("quantize_x", 7), ("quantize_w", 2)]
    vector += [("interleave", 3), ("widen", 2, 3), ("quantize_w", 3)]
    vector += [("interleave", 4), ("widen", 3, 2), ("quantize_w", 4)]
    vector += [("interleave", 5), ("widen", 3, 3), ("quantize_w", 5)]
    vector += [("interleave", 6), ("interleave", 7), ("quantize_w", 6), ("quantize_w", 7)]
    vector += steps("finish", range(TILES))

    scalar = [("widen", 0, 0)] + both_halves("empty", (0, 1))
    scalar += [("widen", 1, 0)] + both_halves("empty", (2, 3))
    scalar += [("widen", 1, 1)] + both_halves("empty", (4,))
    scalar += [("widen", 1, 2)] + both_halves("empty", (5, 6, 7))
    scalar += [("widen", 2, 0), ("widen", 2, 1), ("widen", 2, 2), ("widen", 3, 0), ("widen", 3, 1)]
    scalar += steps("keep_low", range(TILES))

    tensor = both_halves("transpose", range(4)) + passes((0,), (0, 1))
    tensor += both_halves("transpose", (4, 5)) + passes((0,), (2, 3))
    tensor += both_halves("transpose", (6,)) + passes((1,), (0, 1))
    tensor += both_halves("transpose", (7,)) + passes((1,), (2, 3))
    tensor += [("multiply", e, i) for i in range(4, TILES) for e in (0, 1)]
    tensor += passes((2, 3), range(TILES))
    tensor += in_turn(4, 4) + in_turn(6, 1)

    return {VECTOR: vector, SCALAR: scalar, TENSOR: tensor, GPSIMD: [("bucket", 3)]}


def needs(step):
    kind = step[0]
    if kind == "interleave":
        return [("widen", step[1] // 2, t) for t in range(PACK)]
    if kind == "quantize_w":
        return [("interleave", step[1])]
    if kind == "bucket":
        return [] if step[1] == 0 else [("bucket", 0)] if step[1] in (1, 3) else [("bucket", 1)]
    if kind == "mask":
        return [("bucket", 2)]
    if kind == "transpose":
        before = 2 * step[1] + step[2] - len(TRANSPOSE_BANKS)
        return [("mask", step[1])] + [("empty", b // 2, b % 2) for b in (before, before + 1 - step[2]) if b >= 0]
    if kind == "empty":
        return [("transpose", step[1], step[2])]
    if kind == "quantize_x":
        return [("empty", step[1], 0), ("empty", step[1], 1)]
    if kind == "multiply":
        e, i = step[1], step[2]
        before = [("quantize_x", i), ("quantize_w", e)]
        if e < GROUPS and i in TRANSPOSE_BANKS:
            last = [b for b in range(2 * TILES) if TRANSPOSE_BANKS[b % len(TRANSPOSE_BANKS)] == i][-1]
            before.append(("empty", last // 2, last % 2))
        if e >= GROUPS:
            before.append(("keep_low", i))
        return before
    if kind == "keep_low":
        return [("multiply", e, step[1]) for e in range(GROUPS)] + [("bucket", 3)]
    if kind == "finish":
        return [("multiply", e, step[1]) for e in range(GROUPS, EXPERTS)] + [("keep_low", step[1])]
    return []


def text_order(queues):
    position = {}
    for engine in queues:
        position[engine] = 0
    written = set()
    text = []
    total = sum(len(queues[engine]) for engine in queues)
    for rounds in range(total):
        for engine in queues:
            for tries in range(len(queues[engine])):
                if position[engine] >= len(queues[engine]):
                    break
                step = queues[engine][position[engine]]
                if not all(n in written for n in needs(step)):
                    break
                text.append((engine, step))
                written.add(step)
                position[engine] = position[engine] + 1
    assert len(text) == total, "the queues block each other"
    return text


def tile_dispatchbyvariable_pa_kernel(tc, x, W_bytes, W_scale, out):
    nc = tc.nc
    with ExitStack() as ctx:
        keep = ctx.enter_context(tc.tile_pool(name="keep", bufs=1))
        psum = ctx.enter_context(tc.psum_pool(name="psum", bufs=1))
        ctx.enter_context(tc.manual_schedule())

        w_scale = keep.tile([P, PACK], F32, name="w_scale")
        w_bytes = []
        for q in range(PAIRS):
            w_bytes_q = keep.tile([P, PACK, 2, F], U8, name="w_bytes%d" % q)
            w_bytes.append(w_bytes_q)
        x_rows = keep.tile([P, TILES, D], BF16, name="x_rows")
        x_view = x.rearrange("b t d -> (b t) d").rearrange("(i p) d -> p i d", p=P)
        feature = keep.tile([P, TILES, FEATURE_ROW], BF16, name="feature")

        def load_x(j):
            nc.sync.dma_start(out=x_rows[:, 2 * j : 2 * j + 2, :], in_=x_view[:, 2 * j : 2 * j + 2, :])

        def load_w(e):
            nc.sync.dma_start(
                out=w_bytes[e // 2][:, :, e % 2, :], in_=W_bytes[e].rearrange("(p t) n -> p t n", t=PACK)
            )

        nc.sync.dma_start(out=feature[:], in_=x_view[:, :, 0:FEATURE_ROW])
        load_x(0)
        nc.sync.dma_start(out=w_scale[:], in_=W_scale.rearrange("o (p t) u -> p (o t u)", t=PACK))
        first_pair = W_bytes[0:2].rearrange("e (p t) n -> p t e n", t=PACK)
        for t in range(PACK):
            nc.sync.dma_start(out=w_bytes[0][:, t, :, :], in_=first_pair[:, t, :, :])
        for j in range(1, TILES // 2):
            load_x(j)
            load_w(2 * j)
            load_w(2 * j + 1)

        col_minus_row = keep.tile([P, GROUPS * P], I32, name="col_minus_row")
        nc.gpsimd.iota(col_minus_row[:], pattern=[[1, GROUPS * P]], base=0, channel_multiplier=-1)
        boundaries = keep.tile([P, len(BOUNDARIES)], F32, name="boundaries")
        for j in range(len(BOUNDARIES)):
            nc.vector.memset(boundaries[:, j : j + 1], BOUNDARIES[j])
        table_load = keep.tile([P, 1], F32, name="table_load")
        nc.scalar.activation(out=table_load[:], in_=boundaries[:, 0:1], func=ACT.Copy)
        block_of_col = keep.tile([P, GROUPS * P], F32, name="block_of_col")
        nc.vector.tensor_scalar(out=block_of_col[:], in0=col_minus_row[:], scalar1=1.0 / P, scalar2=None, op0=ALU.mult)

        w_planes = []
        for q in range(PAIRS):
            w_planes_q = keep.tile([P, PACK, 2, F], BF16, name="w_planes%d" % q)
            w_planes.append(w_planes_q)
        w_grouped = []
        w_codes = []
        w_scales = []
        for e in range(EXPERTS):
            w_grouped_e = keep.tile([P, PACK * F], BF16, name="w_grouped%d" % e, align_bytes=64)
            w_codes_e = keep.tile([P, F], U32, name="w_codes%d" % e, align_bytes=64)
            w_scales_e = keep.tile([P, F], U8, name="w_scales%d" % e, align_bytes=64)
            w_grouped.append(w_grouped_e)
            w_codes.append(w_codes_e)
            w_scales.append(w_scales_e)

        def widen(engine, q, t):
            codes = w_bytes[q][:, t, :, :].rearrange("p e n -> p (e n)").bitcast(FP8)
            values = w_planes[q][:, t, :, :].rearrange("p e n -> p (e n)")
            if engine == VECTOR:
                nc.vector.tensor_scalar(out=values, in0=codes, scalar1=w_scale[:, t : t + 1], scalar2=None, op0=ALU.mult)
            else:
                nc.scalar.activation(out=values, in_=codes, func=ACT.Copy, scale=w_scale[:, t : t + 1])

        def interleave(e):
            nc.vector.tensor_copy(
                out=w_grouped[e][:].rearrange("p (c i t) -> p c t i", i=4, t=PACK),
                in_=w_planes[e // 2][:, :, e % 2, :].rearrange("p t (c i) -> p c t i", i=4),
            )

        def quantize_w(e):
            nc.vector.quantize_mx(out=w_codes[e][:].bitcast(FP8X4), scales=w_scales[e][:], in_=w_grouped[e][:])

        above = keep.tile([P, TILES, len(BOUNDARIES)], F32, name="above")
        m_count = keep.tile([P, TILES], F32, name="m_count")
        group = keep.tile([P, TILES], F32, name="group")
        low = keep.tile([P, TILES], F32, name="low")
        masked_identity = []
        x_grouped = []
        x_codes = []
        x_scales = []
        for i in range(TILES):
            masked_identity_i = keep.tile([P, GROUPS * P], F32, name="masked_identity%d" % i)
            x_grouped_i = keep.tile([P, GROUPS * P * PACK], BF16, name="x_grouped%d" % i, align_bytes=64)
            x_codes_i = keep.tile([P, GROUPS * P], U32, name="x_codes%d" % i, align_bytes=64)
            x_scales_i = keep.tile([P, GROUPS * P], U8, name="x_scales%d" % i, align_bytes=64)
            masked_identity.append(masked_identity_i)
            x_grouped.append(x_grouped_i)
            x_codes.append(x_codes_i)
            x_scales.append(x_scales_i)
        x_words = x_rows[:].rearrange("p i d -> p (i d)").bitcast(F32)
        high = above[:, :, ZERO_BOUNDARY]

        def bucket(k):
            if k == 0:
                nc.vector.tensor_tensor(
                    out=above[:],
                    in0=feature[:, :, 0:1].to_broadcast([P, TILES, len(BOUNDARIES)]),
                    in1=boundaries[:].unsqueeze(1).to_broadcast([P, TILES, len(BOUNDARIES)]),
                    op=ALU.is_gt,
                )
            elif k == 1:
                nc.vector.tensor_reduce(out=m_count[:], in_=above[:], axis=AX.X, op=ALU.add)
            elif k == 2:
                nc.vector.scalar_tensor_tensor(
                    out=group[:], in0=high, scalar=-float(GROUPS), in1=m_count[:], op0=ALU.mult, op1=ALU.add
                )
            else:
                nc.gpsimd.tensor_scalar(out=low[:], in0=high, scalar1=-1.0, scalar2=1.0, op0=ALU.mult, op1=ALU.add)

        def mask(i):
            nc.vector.tensor_scalar(
                out=masked_identity[i][:], in0=block_of_col[:], scalar1=group[:, i : i + 1], scalar2=None, op0=ALU.is_equal
            )

        turned = {}

        def transpose(i, h):
            bank = psum.tile(
                [P, 2, 2, P],
                F32,
                name="turned%d_%d" % (i, h),
                tag="bank%d" % TRANSPOSE_BANKS[(2 * i + h) % len(TRANSPOSE_BANKS)],
            )
            turned[(i, h)] = bank
            for a in (2 * h, 2 * h + 1):
                for u in range(2):
                    nc.tensor.transpose(
                        bank[:, a - 2 * h, u, :],
                        x_words[:, TOKEN_WORDS * i + u : TOKEN_WORDS * (i + 1) : 2],
                        masked_identity[i][:, P * a : P * (a + 1)],
                    )

        def empty(i, h):
            words = x_grouped[i][:].bitcast(F32)
            nc.scalar.copy(
                out=words[:, HALF_WORDS * h : HALF_WORDS * (h + 1)].rearrange("p (a r u) -> p a r u", a=2, u=2),
                in_=turned[(i, h)][:].rearrange("p a u r -> p a r u"),
            )

        def quantize_x(i):
            nc.vector.quantize_mx(out=x_codes[i][:].bitcast(FP8X4), scales=x_scales[i][:], in_=x_grouped[i][:])

        sums = {}
        done = {}

        def multiply(e, i):
            sweep = e // GROUPS
            n = done.get((sweep, i), 0)
            done[(sweep, i)] = n + 1
            if n == 0:
                sums_i = psum.tile([P, F], F32, name="sums%d_%d" % (sweep, i), tag="bank%d" % i)
                sums[i] = sums_i
            cols = slice(P * (e % GROUPS), P * (e % GROUPS + 1))
            nc.tensor.matmul_mx(
                out=sums[i][:],
                lhsT=x_codes[i][:, cols].bitcast(FP8X4),
                lhsT_scale=x_scales[i][:, cols],
                rhs=w_codes[e][:].bitcast(FP8X4),
                rhs_scale=w_scales[e][:],
                start=(n == 0),
                stop=(n == GROUPS - 1),
            )

        low_part = {}
        out_view = out.rearrange("b t f -> (b t) f").rearrange("(i p) f -> p i f", p=P)

        def keep_low(i):
            low_part_i = keep.tile([P, F], F32, name="low_part%d" % i)
            low_part[i] = low_part_i
            nc.scalar.activation(out=low_part_i[:], in_=sums[i][:], func=ACT.Copy, scale=low[:, i : i + 1])

        def finish(i):
            result_i = keep.tile([P, F], F32, name="result%d" % i)
            nc.vector.scalar_tensor_tensor(
                out=result_i[:],
                in0=sums[i][:],
                scalar=above[:, i, ZERO_BOUNDARY : ZERO_BOUNDARY + 1],
                in1=low_part[i][:],
                op0=ALU.mult,
                op1=ALU.add,
            )
            nc.sync.dma_start(out=out_view[:, i, :], in_=result_i[:])

        for engine, step in text_order(engine_queues()):
            kind = step[0]
            if kind == "widen":
                widen(engine, step[1], step[2])
            elif kind == "interleave":
                interleave(step[1])
            elif kind == "quantize_w":
                quantize_w(step[1])
            elif kind == "bucket":
                bucket(step[1])
            elif kind == "mask":
                mask(step[1])
            elif kind == "transpose":
                transpose(step[1], step[2])
            elif kind == "empty":
                empty(step[1], step[2])
            elif kind == "quantize_x":
                quantize_x(step[1])
            elif kind == "multiply":
                multiply(step[1], step[2])
            elif kind == "keep_low":
                keep_low(step[1])
            else:
                finish(step[1])
